import numpy as np
import ml_dtypes


def mxq(x, axis, fmt="e4m3"):
    dtype, down = {"e4m3": (ml_dtypes.float8_e4m3fn, 7), "e5m2": (ml_dtypes.float8_e5m2, 14)}[fmt]
    v = np.moveaxis(np.asarray(x, np.float32).astype(ml_dtypes.bfloat16).astype(np.float64), axis, -1)
    blocks = v.reshape(v.shape[:-1] + (-1, 32))
    amax = np.abs(blocks).max(-1, keepdims=True)
    byte = np.maximum(np.where(amax > 0, np.frexp(amax)[1] - 1 + 127, 0) - down, 1)
    scale = np.exp2(byte - 127.0)
    codes = (blocks / scale).astype(np.float32).astype(dtype).astype(np.float64)
    return np.moveaxis((codes * scale).reshape(v.shape), -1, axis)


WIDE = False


def mx_kscale(k):
    if not WIDE:
        return np.ones(k)
    levels = np.array([10, -10, 5, -5, 0])
    a = np.random.permutation(np.resize(levels, k // 512 * 4)).reshape(k // 512, 4)
    idx = np.arange(k)
    return np.exp2(a[idx // 512, idx % 128 // 32])


BF16 = ml_dtypes.bfloat16


def bf(x):
    return np.asarray(x, np.float32).astype(BF16)


def f64(x):
    return np.asarray(x).astype(np.float64)


B, L0, W0, R, DIM, OUT = 4096, 16, 8, 32, 512, 128
K1 = L0 * W0
KR = R * R
EPS = 1e-5


def setup_inputs():
    s2, s3 = mx_kscale(KR), mx_kscale(KR)
    rn = np.random.standard_normal
    return {
        "x": bf(rn((B, L0, W0))),
        "km1": bf(rn((L0, W0, DIM)) / np.sqrt(K1)),
        "b1": bf(0.5 + 0.3 * rn(DIM)),
        "t2": bf(rn((B, R, R)) * s2.reshape(R, R)),
        "core2": bf(rn((R, R, DIM)) / np.sqrt(KR) / s2.reshape(R, R, 1)),
        "t3": bf(rn((B, R, R)) * s3.reshape(R, R)),
        "core3": bf(rn((R, R, DIM)) / np.sqrt(KR) / s3.reshape(R, R, 1)),
        "ln_g": bf(1.0 + 0.1 * rn(DIM)),
        "ln_b": bf(0.1 * rn(DIM)),
        "fc_w": bf(rn((OUT, DIM)) / np.sqrt(DIM)),
        "fc_b": bf(0.3 * rn(OUT)),
    }


def reference(x, km1, b1, t2, core2, t3, core3, ln_g, ln_b, fc_w, fc_b):
    o = f64(x).reshape(B, K1) @ f64(km1).reshape(K1, DIM) + f64(b1)
    o = o + (mxq(f64(t2).reshape(B, KR), 1, "e4m3") @ mxq(f64(core2).reshape(KR, DIM), 0, "e4m3"))
    o = o + (mxq(f64(t3).reshape(B, KR), 1, "e4m3") @ mxq(f64(core3).reshape(KR, DIM), 0, "e4m3"))
    mu = o.mean(-1, keepdims=True)
    var = ((o - mu) ** 2).mean(-1, keepdims=True)
    y = (o - mu) / np.sqrt(var + EPS) * f64(ln_g) + f64(ln_b)
    out = (mxq(y, 1, "e4m3") @ mxq(f64(fc_w), 1, "e4m3").T) + f64(fc_b)
    return out[:, None, :]

@@ -1,0 +1,284 @@
+from contextlib import ExitStack
+
+import concourse.mybir as mybir
+from concourse.masks import make_identity
+
+F32 = mybir.dt.float32
+BF16 = mybir.dt.bfloat16
+U32 = mybir.dt.uint32
+U8 = mybir.dt.uint8
+FP8X4 = mybir.dt.float8_e4m3fn_x4
+ALU = mybir.AluOpType
+ACT = mybir.ActivationFunctionType
+
+P = 128
+PACK = 4
+B, K1, KR, DIM, OUT = 4096, 128, 1024, 512, 128
+EPS = 1e-5
+TILES = B // P
+PAIR = 2
+ROUNDS = TILES // PAIR
+CHUNK = 4
+CHUNKS = TILES // CHUNK
+CHUNK_BUFS = 5
+PASSES = 2 * KR // (P * PACK)
+
+FLOPS = 2 * B * DIM * (K1 + 2 * KR) + 2 * B * DIM * OUT
+
+
+def tile_pinmodel_pa_t_kernel(tc, x, km1, b1, t2, core2, t3, core3, ln_g, ln_b, fc_w, fc_b, out):
+    nc = tc.nc
+
+    x_rows = x.rearrange("(p n) i j -> p n (i j)", n=TILES)
+    t_rows = [t.rearrange("(p n) i j -> p n (i j)", n=TILES) for t in (t2, t3)]
+    out_rows = out.rearrange("(p n) o f -> p n (o f)", n=TILES)
+    core_rows = [
+        c.rearrange("i j d -> (i j) d").rearrange("(g u p e) d -> p g u e d", g=2, u=2, e=2) for c in (core2, core3)
+    ]
+
+    with ExitStack() as stack:
+        consts = stack.enter_context(tc.tile_pool(name="consts", bufs=1))
+        chunks = stack.enter_context(tc.tile_pool(name="chunks", bufs=CHUNK_BUFS))
+        stage = stack.enter_context(tc.tile_pool(name="stage", bufs=2))
+        tq = stack.enter_context(tc.tile_pool(name="tq", bufs=6))
+        work = stack.enter_context(tc.tile_pool(name="work", bufs=6))
+        small = stack.enter_context(tc.tile_pool(name="small", bufs=4))
+        yq = stack.enter_context(tc.tile_pool(name="yq", bufs=3))
+        psum_t = stack.enter_context(tc.psum_pool(name="psum_t", bufs=3))
+        psum_z = stack.enter_context(tc.psum_pool(name="psum_z", bufs=2))
+        psum_o = stack.enter_context(tc.psum_pool(name="psum_o", bufs=2))
+        psum_x = stack.enter_context(tc.psum_pool(name="psum_x", bufs=1))
+
+        t_chunks = [[None] * CHUNKS, [None] * CHUNKS]
+
+        def load_chunk(w, c):
+            t_chunk = chunks.tile([P, CHUNK, KR], BF16, tag="t%d" % w, name="t%d_%d" % (w, c))
+            nc.sync.dma_start(out=t_chunk[:], in_=t_rows[w][:, CHUNK * c : CHUNK * (c + 1), :])
+            t_chunks[w][c] = t_chunk
+
+        core_raw = [consts.tile([P, 2, PACK, DIM], BF16, name="core_raw%d" % w) for w in range(2)]
+        x_sb = consts.tile([P, TILES, K1], BF16)
+        for w in range(2):
+            nc.sync.dma_start(out=core_raw[w][:].rearrange("p g (u e) d -> p g u e d", e=2), in_=core_rows[w])
+            load_chunk(w, 0)
+        nc.sync.dma_start(out=x_sb[:], in_=x_rows)
+        for c in range(1, CHUNK_BUFS):
+            for w in range(2):
+                load_chunk(w, c)
+
+        km1_sb = consts.tile([P, DIM], BF16)
+        nc.scalar.dma_start(out=km1_sb[:], in_=km1.rearrange("i j d -> (i j) d"))
+        fcw_sb = consts.tile([P, DIM], BF16)
+        nc.scalar.dma_start(out=fcw_sb[:], in_=fc_w)
+        vec_rows = consts.tile([P, DIM + OUT], BF16)
+        nc.vector.memset(vec_rows[:], 0.0)
+        nc.scalar.dma_start(out=vec_rows[0:1, 0:DIM], in_=b1.rearrange("(o n) -> o n", o=1))
+        nc.scalar.dma_start(out=vec_rows[0:1, DIM : DIM + OUT], in_=fc_b.rearrange("(o n) -> o n", o=1))
+        gb_rows = consts.tile([P, P], BF16)
+        nc.vector.memset(gb_rows[:], 0.0)
+        nc.scalar.dma_start(out=gb_rows[0:PACK, :], in_=ln_g.rearrange("(t p) -> t p", p=P))
+        nc.scalar.dma_start(out=gb_rows[PACK : 2 * PACK, :], in_=ln_b.rearrange("(t p) -> t p", p=P))
+
+        ident_f32 = consts.tile([P, P], F32)
+        make_identity(nc, ident_f32[:])
+        ident_bf = consts.tile([P, P], BF16)
+        make_identity(nc, ident_bf[:])
+        ones = consts.tile([P, P], BF16)
+        nc.vector.memset(ones[:], 1.0)
+        eps_col = consts.tile([P, 1], F32)
+        nc.vector.memset(eps_col[:], EPS)
+
+        core_codes = consts.tile([P, PASSES, DIM], U32, align_bytes=64)
+        core_scales = consts.tile([P, PASSES, DIM], U8, align_bytes=64)
+        for w in range(2):
+            for g in range(2):
+                rows = core_raw[w][:, g].rearrange("p t d -> p d t")
+                core_grouped = stage.tile([P, DIM, PACK], BF16, align_bytes=64)
+                if g == 0:
+                    nc.vector.tensor_copy(out=core_grouped[:], in_=rows)
+                else:
+                    nc.scalar.copy(out=core_grouped[:], in_=rows)
+                nc.vector.quantize_mx(
+                    out=core_codes[:, 2 * w + g, :].bitcast(FP8X4),
+                    scales=core_scales[:, 2 * w + g, :],
+                    in_=core_grouped[:].rearrange("p d t -> p (d t)"),
+                )
+
+        t_codes = {}
+
+        def quantise_t(n):
+            c, slot = divmod(n, CHUNK)
+            t_grouped = stage.tile([P, 2, 2, P, PACK], BF16, align_bytes=64)
+            for w in range(2):
+                words = t_chunks[w][c][:].bitcast(F32)
+                bank = psum_t.tile([P, 4, P], F32, tag="t")
+                for q in range(4):
+                    nc.tensor.transpose(bank[:, q, :], words[:, slot, P * q : P * (q + 1)], ident_f32[:])
+                nc.scalar.copy(
+                    out=t_grouped[:].bitcast(F32)[:, w],
+                    in_=bank[:].rearrange("p (g u) r -> p g r u", u=2),
+                )
+            codes = tq.tile([P, PASSES, P], U32, align_bytes=64)
+            scales = tq.tile([P, PASSES, P], U8, align_bytes=64)
+            nc.vector.quantize_mx(
+                out=codes[:].rearrange("p c r -> p (c r)").bitcast(FP8X4),
+                scales=scales[:].rearrange("p c r -> p (c r)"),
+                in_=t_grouped[:].rearrange("p w g r t -> p (w g r t)"),
+            )
+            t_codes[n] = (codes, scales)
+
+        xT = consts.tile([P, TILES, P], BF16)
+        for m in range(TILES // 8):
+            bank = psum_t.tile([P, 8, P], BF16, tag="t")
+            for i in range(8):
+                nc.tensor.transpose(bank[:, i, :], x_sb[:, 8 * m + i, :], ident_bf[:])
+            nc.scalar.copy(out=xT[:, 8 * m : 8 * m + 8, :], in_=bank[:])
+
+        b1_ps = psum_o.tile([P, DIM], F32, tag="o")
+        nc.tensor.matmul(b1_ps[:], lhsT=ones[:], rhs=vec_rows[:, 0:DIM], start=True, stop=True)
+        b1_bc = consts.tile([P, DIM], F32)
+        nc.vector.tensor_copy(out=b1_bc[:], in_=b1_ps[:])
+        fcb_ps = psum_o.tile([P, OUT], F32, tag="o")
+        nc.tensor.matmul(fcb_ps[:], lhsT=ones[:], rhs=vec_rows[:, DIM : DIM + OUT], start=True, stop=True)
+        fcb_bc = consts.tile([P, OUT], F32)
+        nc.vector.tensor_copy(out=fcb_bc[:], in_=fcb_ps[:])
+
+        gb_ps = psum_z.tile([P, P], BF16, tag="z")
+        nc.tensor.transpose(gb_ps[:], gb_rows[:], ident_bf[:])
+        gb_col = consts.tile([P, 2 * PACK], F32)
+        nc.vector.tensor_copy(out=gb_col[:], in_=gb_ps[:, 0 : 2 * PACK])
+
+        w_ps = psum_z.tile([P, PACK, OUT], BF16, tag="z")
+        for t in range(PACK):
+            nc.tensor.transpose(w_ps[:, t, :], fcw_sb[:, P * t : P * (t + 1)], ident_bf[:])
+        w_grouped = consts.tile([P, OUT, PACK], BF16, align_bytes=64)
+        nc.vector.tensor_copy(out=w_grouped[:], in_=w_ps[:].rearrange("p t o -> p o t"))
+        w_codes = consts.tile([P, OUT], U32, align_bytes=64)
+        w_scales = consts.tile([P, OUT], U8, align_bytes=64)
+        nc.vector.quantize_mx(
+            out=w_codes[:].bitcast(FP8X4), scales=w_scales[:], in_=w_grouped[:].rearrange("p o t -> p (o t)")
+        )
+
+        o_tiles = {}
+        stats = {}
+
+        def sums(j):
+            o_sum = small.tile([P, PAIR], F32)
+            for m in range(PAIR):
+                n = PAIR * j + m
+                xk = psum_x.tile([P, DIM], F32, tag="x")
+                nc.tensor.matmul(xk[:], lhsT=xT[:, n, :], rhs=km1_sb[:], start=True, stop=True)
+                xkb = work.tile([P, DIM], F32)
+                nc.vector.tensor_tensor(out=xkb[:], in0=xk[:], in1=b1_bc[:], op=ALU.add)
+                codes, scales = t_codes[n]
+                acc = psum_o.tile([P, DIM], F32, tag="o")
+                for c in range(PASSES):
+                    nc.tensor.matmul_mx(
+                        out=acc[:],
+                        lhsT=codes[:, c, :].bitcast(FP8X4),
+                        lhsT_scale=scales[:, c, :],
+                        rhs=core_codes[:, c, :].bitcast(FP8X4),
+                        rhs_scale=core_scales[:, c, :],
+                        start=(c == 0),
+                        stop=(c == PASSES - 1),
+                    )
+                o = work.tile([P, DIM], F32)
+                nc.vector.scalar_tensor_tensor(
+                    out=o[:], in0=acc[:], scalar=0.0, in1=xkb[:], op0=ALU.add, op1=ALU.add,
+                    accum_out=o_sum[:, m : m + 1],
+                )
+                o_tiles[n] = o
+            neg_mean = small.tile([P, PAIR], F32)
+            nc.vector.tensor_scalar_mul(out=neg_mean[:], in0=o_sum[:], scalar1=-1.0 / DIM)
+            sq_sum = small.tile([P, PAIR], F32)
+            for m in range(PAIR):
+                squares = work.tile([P, DIM], BF16)
+                nc.scalar.activation(
+                    out=squares[:], in_=o_tiles[PAIR * j + m][:], func=ACT.Square,
+                    bias=neg_mean[:, m : m + 1], scale=1.0, accum_out=sq_sum[:, m : m + 1],
+                )
+            std = small.tile([P, PAIR], F32)
+            nc.scalar.activation(out=std[:], in_=sq_sum[:], func=ACT.Sqrt, bias=eps_col[:], scale=1.0 / DIM)
+            stats[j] = (neg_mean, std)
+
+        z_tiles = {}
+
+        def normalise(j):
+            neg_mean, std = stats[j]
+            rstd = small.tile([P, PAIR], F32)
+            nc.vector.reciprocal(out=rstd[:], in_=std[:])
+            for m in range(PAIR):
+                n = PAIR * j + m
+                z = work.tile([P, DIM], F32)
+                nc.vector.tensor_scalar(
+                    out=z[:], in0=o_tiles[n][:], scalar1=neg_mean[:, m : m + 1], scalar2=rstd[:, m : m + 1],
+                    op0=ALU.add, op1=ALU.mult,
+                )
+                z_tiles[n] = z
+
+        y_codes = {}
+
+        def quantise_y(j):
+            yT = stage.tile([P, PACK, PAIR, P], BF16)
+            for half in range(2):
+                bank = psum_z.tile([P, 2, PAIR, P], F32, tag="z")
+                for tt in range(2):
+                    t = 2 * half + tt
+                    for m in range(PAIR):
+                        nc.tensor.transpose(
+                            bank[:, tt, m, :], z_tiles[PAIR * j + m][:, P * t : P * (t + 1)], ident_f32[:]
+                        )
+                for tt in range(2):
+                    t = 2 * half + tt
+                    nc.scalar.activation(
+                        out=yT[:, t, :, :], in_=bank[:, tt, :, :], func=ACT.Identity,
+                        scale=gb_col[:, t : t + 1], bias=gb_col[:, PACK + t : PACK + t + 1],
+                    )
+            y_grouped = stage.tile([P, PAIR, P, PACK], BF16, align_bytes=64)
+            nc.vector.tensor_copy(out=y_grouped[:], in_=yT[:].rearrange("p t m r -> p m r t"))
+            codes = yq.tile([P, PAIR, P], U32, align_bytes=64)
+            scales = yq.tile([P, PAIR, P], U8, align_bytes=64)
+            nc.vector.quantize_mx(
+                out=codes[:].rearrange("p m r -> p (m r)").bitcast(FP8X4),
+                scales=scales[:].rearrange("p m r -> p (m r)"),
+                in_=y_grouped[:].rearrange("p m r t -> p (m r t)"),
+            )
+            y_codes[j] = (codes, scales)
+
+        def head(j):
+            codes, scales = y_codes[j]
+            fin = psum_x.tile([P, PAIR, OUT], F32, tag="x")
+            for m in range(PAIR):
+                nc.tensor.matmul_mx(
+                    out=fin[:, m, :],
+                    lhsT=codes[:, m, :].bitcast(FP8X4),
+                    lhsT_scale=scales[:, m, :],
+                    rhs=w_codes[:].bitcast(FP8X4),
+                    rhs_scale=w_scales[:],
+                    start=True,
+                    stop=True,
+                )
+            result = yq.tile([P, PAIR, OUT], F32)
+            nc.vector.tensor_tensor(
+                out=result[:], in0=fin[:], in1=fcb_bc[:].unsqueeze(1).to_broadcast([P, PAIR, OUT]), op=ALU.add
+            )
+            nc.sync.dma_start(out=out_rows[:, PAIR * j : PAIR * (j + 1), :], in_=result[:])
+
+        for m in range(PAIR):
+            quantise_t(m)
+        for s in range(ROUNDS + 3):
+            if s + 1 < ROUNDS:
+                for m in range(PAIR):
+                    quantise_t(PAIR * (s + 1) + m)
+                done_chunks, rest = divmod(PAIR * (s + 2), CHUNK)
+                if rest == 0 and done_chunks - 1 + CHUNK_BUFS < CHUNKS:
+                    for w in range(2):
+                        load_chunk(w, done_chunks - 1 + CHUNK_BUFS)
+            if 0 <= s - 2 < ROUNDS:
+                quantise_y(s - 2)
+            if s < ROUNDS:
+                sums(s)
+            if 0 <= s - 1 < ROUNDS:
+                normalise(s - 1)
+            if 0 <= s - 3 < ROUNDS:
+                head(s - 3)

@@ -18,9 +18,7 @@ EPS = 1e-5
 TILES = B // P
 PAIR = 2
 ROUNDS = TILES // PAIR
-CHUNK = 4
-CHUNKS = TILES // CHUNK
-CHUNK_BUFS = 5
+T_BUFS = 8
 PASSES = 2 * KR // (P * PACK)
 
 FLOPS = 2 * B * DIM * (K1 + 2 * KR) + 2 * B * DIM * OUT
@@ -37,9 +35,11 @@ def tile_pinmodel_pa_t_kernel(tc, x, km1, b1, t2, core2, t3, core3, ln_g, ln_b, 
     ]
 
     with ExitStack() as stack:
+        stack.enter_context(tc.manual_schedule())
         consts = stack.enter_context(tc.tile_pool(name="consts", bufs=1))
-        chunks = stack.enter_context(tc.tile_pool(name="chunks", bufs=CHUNK_BUFS))
+        t_pool = stack.enter_context(tc.tile_pool(name="t_pool", bufs=T_BUFS))
         stage = stack.enter_context(tc.tile_pool(name="stage", bufs=2))
+        grouped_pool = stack.enter_context(tc.tile_pool(name="grouped_pool", bufs=6))
         tq = stack.enter_context(tc.tile_pool(name="tq", bufs=6))
         work = stack.enter_context(tc.tile_pool(name="work", bufs=6))
         small = stack.enter_context(tc.tile_pool(name="small", bufs=4))
@@ -49,22 +49,26 @@ def tile_pinmodel_pa_t_kernel(tc, x, km1, b1, t2, core2, t3, core3, ln_g, ln_b, 
         psum_o = stack.enter_context(tc.psum_pool(name="psum_o", bufs=2))
         psum_x = stack.enter_context(tc.psum_pool(name="psum_x", bufs=1))
 
-        t_chunks = [[None] * CHUNKS, [None] * CHUNKS]
+        def live(j):
+            return 0 <= j < ROUNDS
 
-        def load_chunk(w, c):
-            t_chunk = chunks.tile([P, CHUNK, KR], BF16, tag="t%d" % w, name="t%d_%d" % (w, c))
-            nc.sync.dma_start(out=t_chunk[:], in_=t_rows[w][:, CHUNK * c : CHUNK * (c + 1), :])
-            t_chunks[w][c] = t_chunk
+        t_raw = {}
+
+        def load_t(j):
+            if not live(j):
+                return
+            for w in range(2):
+                t_raw[w, j] = t_pool.tile([P, PAIR, KR], BF16, tag="t%d" % w, name="t%d_%d" % (w, j))
+                nc.sync.dma_start(out=t_raw[w, j][:], in_=t_rows[w][:, PAIR * j : PAIR * (j + 1), :])
 
         core_raw = [consts.tile([P, 2, PACK, DIM], BF16, name="core_raw%d" % w) for w in range(2)]
         x_sb = consts.tile([P, TILES, K1], BF16)
         for w in range(2):
             nc.sync.dma_start(out=core_raw[w][:].rearrange("p g (u e) d -> p g u e d", e=2), in_=core_rows[w])
-            load_chunk(w, 0)
+        load_t(0)
         nc.sync.dma_start(out=x_sb[:], in_=x_rows)
-        for c in range(1, CHUNK_BUFS):
-            for w in range(2):
-                load_chunk(w, c)
+        for j in range(1, T_BUFS):
+            load_t(j)
 
         km1_sb = consts.tile([P, DIM], BF16)
         nc.scalar.dma_start(out=km1_sb[:], in_=km1.rearrange("i j d -> (i j) d"))
@@ -88,52 +92,6 @@ def tile_pinmodel_pa_t_kernel(tc, x, km1, b1, t2, core2, t3, core3, ln_g, ln_b, 
         eps_col = consts.tile([P, 1], F32)
         nc.vector.memset(eps_col[:], EPS)
 
-        core_codes = consts.tile([P, PASSES, DIM], U32, align_bytes=64)
-        core_scales = consts.tile([P, PASSES, DIM], U8, align_bytes=64)
-        for w in range(2):
-            for g in range(2):
-                rows = core_raw[w][:, g].rearrange("p t d -> p d t")
-                core_grouped = stage.tile([P, DIM, PACK], BF16, align_bytes=64)
-                if g == 0:
-                    nc.vector.tensor_copy(out=core_grouped[:], in_=rows)
-                else:
-                    nc.scalar.copy(out=core_grouped[:], in_=rows)
-                nc.vector.quantize_mx(
-                    out=core_codes[:, 2 * w + g, :].bitcast(FP8X4),
-                    scales=core_scales[:, 2 * w + g, :],
-                    in_=core_grouped[:].rearrange("p d t -> p (d t)"),
-                )
-
-        t_codes = {}
-
-        def quantise_t(n):
-            c, slot = divmod(n, CHUNK)
-            t_grouped = stage.tile([P, 2, 2, P, PACK], BF16, align_bytes=64)
-            for w in range(2):
-                words = t_chunks[w][c][:].bitcast(F32)
-                bank = psum_t.tile([P, 4, P], F32, tag="t")
-                for q in range(4):
-                    nc.tensor.transpose(bank[:, q, :], words[:, slot, P * q : P * (q + 1)], ident_f32[:])
-                nc.scalar.copy(
-                    out=t_grouped[:].bitcast(F32)[:, w],
-                    in_=bank[:].rearrange("p (g u) r -> p g r u", u=2),
-                )
-            codes = tq.tile([P, PASSES, P], U32, align_bytes=64)
-            scales = tq.tile([P, PASSES, P], U8, align_bytes=64)
-            nc.vector.quantize_mx(
-                out=codes[:].rearrange("p c r -> p (c r)").bitcast(FP8X4),
-                scales=scales[:].rearrange("p c r -> p (c r)"),
-                in_=t_grouped[:].rearrange("p w g r t -> p (w g r t)"),
-            )
-            t_codes[n] = (codes, scales)
-
-        xT = consts.tile([P, TILES, P], BF16)
-        for m in range(TILES // 8):
-            bank = psum_t.tile([P, 8, P], BF16, tag="t")
-            for i in range(8):
-                nc.tensor.transpose(bank[:, i, :], x_sb[:, 8 * m + i, :], ident_bf[:])
-            nc.scalar.copy(out=xT[:, 8 * m : 8 * m + 8, :], in_=bank[:])
-
         b1_ps = psum_o.tile([P, DIM], F32, tag="o")
         nc.tensor.matmul(b1_ps[:], lhsT=ones[:], rhs=vec_rows[:, 0:DIM], start=True, stop=True)
         b1_bc = consts.tile([P, DIM], F32)
@@ -155,97 +113,183 @@ def tile_pinmodel_pa_t_kernel(tc, x, km1, b1, t2, core2, t3, core3, ln_g, ln_b, 
         nc.vector.tensor_copy(out=w_grouped[:], in_=w_ps[:].rearrange("p t o -> p o t"))
         w_codes = consts.tile([P, OUT], U32, align_bytes=64)
         w_scales = consts.tile([P, OUT], U8, align_bytes=64)
-        nc.vector.quantize_mx(
-            out=w_codes[:].bitcast(FP8X4), scales=w_scales[:], in_=w_grouped[:].rearrange("p o t -> p (o t)")
-        )
+
+        core_codes = consts.tile([P, PASSES, DIM], U32, align_bytes=64)
+        core_scales = consts.tile([P, PASSES, DIM], U8, align_bytes=64)
+        for w in range(2):
+            core_grouped = [
+                stage.tile([P, DIM, PACK], BF16, align_bytes=64, tag="core%d" % g, name="core_grouped%d_%d" % (w, g))
+                for g in range(2)
+            ]
+            nc.vector.tensor_copy(out=core_grouped[0][:], in_=core_raw[w][:, 0].rearrange("p t d -> p d t"))
+            nc.scalar.copy(out=core_grouped[1][:], in_=core_raw[w][:, 1].rearrange("p t d -> p d t"))
+            if w == 0:
+                nc.vector.quantize_mx(
+                    out=w_codes[:].bitcast(FP8X4), scales=w_scales[:], in_=w_grouped[:].rearrange("p o t -> p (o t)")
+                )
+            for g in range(2):
+                nc.vector.quantize_mx(
+                    out=core_codes[:, 2 * w + g, :].bitcast(FP8X4),
+                    scales=core_scales[:, 2 * w + g, :],
+                    in_=core_grouped[g][:].rearrange("p d t -> p (d t)"),
+                )
+
+        t_bank = {}
+        t_grouped = {}
+        t_codes = {}
+
+        def transpose_t(j, m, w):
+            if not live(j):
+                return
+            words = t_raw[w, j][:].bitcast(F32)
+            t_bank[j, m, w] = psum_t.tile([P, 4, P], F32, tag="t", name="t_bank")
+            for q in range(4):
+                nc.tensor.transpose(t_bank[j, m, w][:, q, :], words[:, m, P * q : P * (q + 1)], ident_f32[:])
+
+        def copy_t(j, m, w):
+            if not live(j):
+                return
+            if w == 0:
+                t_grouped[j, m] = grouped_pool.tile([P, 2, 2, P, PACK], BF16, align_bytes=64, name="t_grouped")
+            nc.scalar.copy(
+                out=t_grouped[j, m][:].bitcast(F32)[:, w],
+                in_=t_bank[j, m, w][:].rearrange("p (g u) r -> p g r u", u=2),
+            )
+
+        def quantise_t(j, m):
+            if not live(j):
+                return
+            codes = tq.tile([P, PASSES, P], U32, align_bytes=64)
+            scales = tq.tile([P, PASSES, P], U8, align_bytes=64)
+            nc.vector.quantize_mx(
+                out=codes[:].rearrange("p c r -> p (c r)").bitcast(FP8X4),
+                scales=scales[:].rearrange("p c r -> p (c r)"),
+                in_=t_grouped[j, m][:].rearrange("p w g r t -> p (w g r t)"),
+            )
+            t_codes[j, m] = (codes, scales)
+
+        xT = consts.tile([P, TILES, P], BF16)
+        xkb_tiles = {}
+
+        def plain_product(j, m):
+            if not live(j):
+                return
+            xk = psum_x.tile([P, DIM], F32, tag="x")
+            nc.tensor.matmul(xk[:], lhsT=xT[:, PAIR * j + m, :], rhs=km1_sb[:], start=True, stop=True)
+            xkb = work.tile([P, DIM], F32)
+            nc.vector.tensor_tensor(out=xkb[:], in0=xk[:], in1=b1_bc[:], op=ALU.add)
+            xkb_tiles[j, m] = xkb
 
         o_tiles = {}
-        stats = {}
+        o_sums = {}
 
-        def sums(j):
-            o_sum = small.tile([P, PAIR], F32)
-            for m in range(PAIR):
-                n = PAIR * j + m
-                xk = psum_x.tile([P, DIM], F32, tag="x")
-                nc.tensor.matmul(xk[:], lhsT=xT[:, n, :], rhs=km1_sb[:], start=True, stop=True)
-                xkb = work.tile([P, DIM], F32)
-                nc.vector.tensor_tensor(out=xkb[:], in0=xk[:], in1=b1_bc[:], op=ALU.add)
-                codes, scales = t_codes[n]
-                acc = psum_o.tile([P, DIM], F32, tag="o")
-                for c in range(PASSES):
-                    nc.tensor.matmul_mx(
-                        out=acc[:],
-                        lhsT=codes[:, c, :].bitcast(FP8X4),
-                        lhsT_scale=scales[:, c, :],
-                        rhs=core_codes[:, c, :].bitcast(FP8X4),
-                        rhs_scale=core_scales[:, c, :],
-                        start=(c == 0),
-                        stop=(c == PASSES - 1),
-                    )
-                o = work.tile([P, DIM], F32)
-                nc.vector.scalar_tensor_tensor(
-                    out=o[:], in0=acc[:], scalar=0.0, in1=xkb[:], op0=ALU.add, op1=ALU.add,
-                    accum_out=o_sum[:, m : m + 1],
+        def mx_products(j, m):
+            if not live(j):
+                return
+            if m == 0:
+                o_sums[j] = small.tile([P, PAIR], F32, name="o_sum")
+            codes, scales = t_codes[j, m]
+            acc = psum_o.tile([P, DIM], F32, tag="o")
+            for c in range(PASSES):
+                nc.tensor.matmul_mx(
+                    out=acc[:],
+                    lhsT=codes[:, c, :].bitcast(FP8X4),
+                    lhsT_scale=scales[:, c, :],
+                    rhs=core_codes[:, c, :].bitcast(FP8X4),
+                    rhs_scale=core_scales[:, c, :],
+                    start=(c == 0),
+                    stop=(c == PASSES - 1),
                 )
-                o_tiles[n] = o
-            neg_mean = small.tile([P, PAIR], F32)
-            nc.vector.tensor_scalar_mul(out=neg_mean[:], in0=o_sum[:], scalar1=-1.0 / DIM)
+            o = work.tile([P, DIM], F32)
+            nc.vector.scalar_tensor_tensor(
+                out=o[:], in0=acc[:], scalar=0.0, in1=xkb_tiles[j, m][:], op0=ALU.add, op1=ALU.add,
+                accum_out=o_sums[j][:, m : m + 1],
+            )
+            o_tiles[j, m] = o
+
+        neg_means = {}
+        stds = {}
+
+        def mean(j):
+            if not live(j):
+                return
+            neg_means[j] = small.tile([P, PAIR], F32, name="neg_mean")
+            nc.vector.tensor_scalar_mul(out=neg_means[j][:], in0=o_sums[j][:], scalar1=-1.0 / DIM)
+
+        def deviation(j):
+            if not live(j):
+                return
             sq_sum = small.tile([P, PAIR], F32)
             for m in range(PAIR):
-                squares = work.tile([P, DIM], BF16)
+                squares = stage.tile([P, DIM], BF16)
                 nc.scalar.activation(
-                    out=squares[:], in_=o_tiles[PAIR * j + m][:], func=ACT.Square,
-                    bias=neg_mean[:, m : m + 1], scale=1.0, accum_out=sq_sum[:, m : m + 1],
+                    out=squares[:], in_=o_tiles[j, m][:], func=ACT.Square,
+                    bias=neg_means[j][:, m : m + 1], scale=1.0, accum_out=sq_sum[:, m : m + 1],
                 )
-            std = small.tile([P, PAIR], F32)
-            nc.scalar.activation(out=std[:], in_=sq_sum[:], func=ACT.Sqrt, bias=eps_col[:], scale=1.0 / DIM)
-            stats[j] = (neg_mean, std)
+            stds[j] = small.tile([P, PAIR], F32, name="std")
+            nc.scalar.activation(out=stds[j][:], in_=sq_sum[:], func=ACT.Sqrt, bias=eps_col[:], scale=1.0 / DIM)
 
         z_tiles = {}
 
         def normalise(j):
-            neg_mean, std = stats[j]
+            if not live(j):
+                return
             rstd = small.tile([P, PAIR], F32)
-            nc.vector.reciprocal(out=rstd[:], in_=std[:])
+            nc.vector.reciprocal(out=rstd[:], in_=stds[j][:])
             for m in range(PAIR):
-                n = PAIR * j + m
                 z = work.tile([P, DIM], F32)
                 nc.vector.tensor_scalar(
-                    out=z[:], in0=o_tiles[n][:], scalar1=neg_mean[:, m : m + 1], scalar2=rstd[:, m : m + 1],
+                    out=z[:], in0=o_tiles[j, m][:], scalar1=neg_means[j][:, m : m + 1], scalar2=rstd[:, m : m + 1],
                     op0=ALU.add, op1=ALU.mult,
                 )
-                z_tiles[n] = z
+                z_tiles[j, m] = z
 
+        z_bank = {}
+        y_planes = {}
+        y_grouped = {}
         y_codes = {}
 
-        def quantise_y(j):
-            yT = stage.tile([P, PACK, PAIR, P], BF16)
+        def transpose_z(j):
+            if not live(j):
+                return
             for half in range(2):
-                bank = psum_z.tile([P, 2, PAIR, P], F32, tag="z")
+                z_bank[j, half] = psum_z.tile([P, 2, PAIR, P], F32, tag="z", name="z_bank")
                 for tt in range(2):
                     t = 2 * half + tt
                     for m in range(PAIR):
-                        nc.tensor.transpose(
-                            bank[:, tt, m, :], z_tiles[PAIR * j + m][:, P * t : P * (t + 1)], ident_f32[:]
-                        )
-                for tt in range(2):
-                    t = 2 * half + tt
-                    nc.scalar.activation(
-                        out=yT[:, t, :, :], in_=bank[:, tt, :, :], func=ACT.Identity,
-                        scale=gb_col[:, t : t + 1], bias=gb_col[:, PACK + t : PACK + t + 1],
-                    )
-            y_grouped = stage.tile([P, PAIR, P, PACK], BF16, align_bytes=64)
-            nc.vector.tensor_copy(out=y_grouped[:], in_=yT[:].rearrange("p t m r -> p m r t"))
-            codes = yq.tile([P, PAIR, P], U32, align_bytes=64)
-            scales = yq.tile([P, PAIR, P], U8, align_bytes=64)
+                        nc.tensor.transpose(z_bank[j, half][:, tt, m, :], z_tiles[j, m][:, P * t : P * (t + 1)], ident_f32[:])
+
+        def scale_shift(j):
+            if not live(j):
+                return
+            y_planes[j] = stage.tile([P, PACK, PAIR, P], BF16, name="y_planes")
+            for t in range(PACK):
+                nc.scalar.activation(
+                    out=y_planes[j][:, t, :, :], in_=z_bank[j, t // 2][:, t % 2, :, :], func=ACT.Identity,
+                    scale=gb_col[:, t : t + 1], bias=gb_col[:, PACK + t : PACK + t + 1],
+                )
+
+        def regroup_y(j):
+            if not live(j):
+                return
+            y_grouped[j] = stage.tile([P, PAIR, P, PACK], BF16, align_bytes=64, name="y_grouped")
+            nc.vector.tensor_copy(out=y_grouped[j][:], in_=y_planes[j][:].rearrange("p t m r -> p m r t"))
+
+        def quantise_y(j):
+            if not live(j):
+                return
+            codes = yq.tile([P, PAIR, P], U32, align_bytes=64, name="y_code")
+            scales = yq.tile([P, PAIR, P], U8, align_bytes=64, name="y_scale")
             nc.vector.quantize_mx(
                 out=codes[:].rearrange("p m r -> p (m r)").bitcast(FP8X4),
                 scales=scales[:].rearrange("p m r -> p (m r)"),
-                in_=y_grouped[:].rearrange("p m r t -> p (m r t)"),
+                in_=y_grouped[j][:].rearrange("p m r t -> p (m r t)"),
             )
             y_codes[j] = (codes, scales)
 
         def head(j):
+            if not live(j):
+                return
             codes, scales = y_codes[j]
             fin = psum_x.tile([P, PAIR, OUT], F32, tag="x")
             for m in range(PAIR):
@@ -265,20 +309,48 @@ def tile_pinmodel_pa_t_kernel(tc, x, km1, b1, t2, core2, t3, core3, ln_g, ln_b, 
             nc.sync.dma_start(out=out_rows[:, PAIR * j : PAIR * (j + 1), :], in_=result[:])
 
         for m in range(PAIR):
-            quantise_t(m)
-        for s in range(ROUNDS + 3):
-            if s + 1 < ROUNDS:
-                for m in range(PAIR):
-                    quantise_t(PAIR * (s + 1) + m)
-                done_chunks, rest = divmod(PAIR * (s + 2), CHUNK)
-                if rest == 0 and done_chunks - 1 + CHUNK_BUFS < CHUNKS:
-                    for w in range(2):
-                        load_chunk(w, done_chunks - 1 + CHUNK_BUFS)
-            if 0 <= s - 2 < ROUNDS:
-                quantise_y(s - 2)
-            if s < ROUNDS:
-                sums(s)
-            if 0 <= s - 1 < ROUNDS:
-                normalise(s - 1)
-            if 0 <= s - 3 < ROUNDS:
-                head(s - 3)
+            for w in range(2):
+                transpose_t(0, m, w)
+                copy_t(0, m, w)
+        load_t(T_BUFS)
+        for m in range(PAIR):
+            quantise_t(0, m)
+        for i in range(TILES // 8):
+            x_bank = psum_t.tile([P, 8, P], BF16, tag="t")
+            for n in range(8 * i, 8 * i + 8):
+                nc.tensor.transpose(x_bank[:, n - 8 * i, :], x_sb[:, n, :], ident_bf[:])
+            nc.scalar.copy(out=xT[:, 8 * i : 8 * i + 8, :], in_=x_bank[:])
+        for m in range(PAIR):
+            for w in range(2):
+                transpose_t(1, m, w)
+                copy_t(1, m, w)
+        load_t(1 + T_BUFS)
+        for m in range(PAIR):
+            plain_product(0, m)
+
+        for s in range(ROUNDS + 4):
+            quantise_t(s + 1, 0)
+            regroup_y(s - 3)
+            quantise_t(s + 1, 1)
+            quantise_y(s - 3)
+
+            transpose_t(s + 2, 0, 0)
+            copy_t(s + 2, 0, 0)
+            transpose_t(s + 2, 0, 1)
+            copy_t(s + 2, 0, 1)
+            transpose_t(s + 2, 1, 0)
+            transpose_z(s - 2)
+            transpose_t(s + 2, 1, 1)
+            load_t(s + 2 + T_BUFS)
+            deviation(s - 1)
+            copy_t(s + 2, 1, 0)
+            copy_t(s + 2, 1, 1)
+            scale_shift(s - 2)
+
+            plain_product(s + 1, 0)
+            mx_products(s, 0)
+            plain_product(s + 1, 1)
+            normalise(s - 1)
+            mx_products(s, 1)
+            mean(s)
+            head(s - 3)

@@ -89,8 +89,8 @@ def tile_pinmodel_pa_t_kernel(tc, x, km1, b1, t2, core2, t3, core3, ln_g, ln_b, 
         make_identity(nc, ident_bf[:])
         ones = consts.tile([P, P], BF16)
         nc.vector.memset(ones[:], 1.0)
-        eps_col = consts.tile([P, 1], F32)
-        nc.vector.memset(eps_col[:], EPS)
+        minus_half = consts.tile([P, PAIR], F32)
+        nc.vector.memset(minus_half[:], -0.5)
 
         b1_ps = psum_o.tile([P, DIM], F32, tag="o")
         nc.tensor.matmul(b1_ps[:], lhsT=ones[:], rhs=vec_rows[:, 0:DIM], start=True, stop=True)
@@ -208,37 +208,41 @@ def tile_pinmodel_pa_t_kernel(tc, x, km1, b1, t2, core2, t3, core3, ln_g, ln_b, 
             o_tiles[j, m] = o
 
         neg_means = {}
-        stds = {}
+        sq_sums = {}
 
         def mean(j):
             if not live(j):
                 return
             neg_means[j] = small.tile([P, PAIR], F32, name="neg_mean")
-            nc.vector.tensor_scalar_mul(out=neg_means[j][:], in0=o_sums[j][:], scalar1=-1.0 / DIM)
+            nc.gpsimd.tensor_scalar(
+                out=neg_means[j][:], in0=o_sums[j][:], scalar1=-1.0 / DIM, scalar2=0.0, op0=ALU.mult, op1=ALU.add
+            )
 
         def deviation(j):
             if not live(j):
                 return
-            sq_sum = small.tile([P, PAIR], F32)
+            sq_sums[j] = small.tile([P, PAIR], F32, name="sq_sum")
             for m in range(PAIR):
                 squares = stage.tile([P, DIM], BF16)
                 nc.scalar.activation(
                     out=squares[:], in_=o_tiles[j, m][:], func=ACT.Square,
-                    bias=neg_means[j][:, m : m + 1], scale=1.0, accum_out=sq_sum[:, m : m + 1],
+                    bias=neg_means[j][:, m : m + 1], scale=1.0, accum_out=sq_sums[j][:, m : m + 1],
                 )
-            stds[j] = small.tile([P, PAIR], F32, name="std")
-            nc.scalar.activation(out=stds[j][:], in_=sq_sum[:], func=ACT.Sqrt, bias=eps_col[:], scale=1.0 / DIM)
 
         z_tiles = {}
 
         def normalise(j):
             if not live(j):
                 return
+            var_eps = small.tile([P, PAIR], F32)
+            nc.gpsimd.tensor_scalar(
+                out=var_eps[:], in0=sq_sums[j][:], scalar1=1.0 / DIM, scalar2=EPS, op0=ALU.mult, op1=ALU.add
+            )
             rstd = small.tile([P, PAIR], F32)
-            nc.vector.reciprocal(out=rstd[:], in_=stds[j][:])
+            nc.gpsimd.tensor_tensor(out=rstd[:], in0=var_eps[:], in1=minus_half[:], op=ALU.pow)
             for m in range(PAIR):
                 z = work.tile([P, DIM], F32)
-                nc.vector.tensor_scalar(
+                nc.gpsimd.tensor_scalar(
                     out=z[:], in0=o_tiles[j, m][:], scalar1=neg_means[j][:, m : m + 1], scalar2=rstd[:, m : m + 1],
                     op0=ALU.add, op1=ALU.mult,
                 )

@@ -19,6 +19,7 @@ TILES = B // P
 PAIR = 2
 ROUNDS = TILES // PAIR
 T_BUFS = 8
+X_BANK = 8
 PASSES = 2 * KR // (P * PACK)
 
 FLOPS = 2 * B * DIM * (K1 + 2 * KR) + 2 * B * DIM * OUT
@@ -62,13 +63,18 @@ def tile_pinmodel_pa_t_kernel(tc, x, km1, b1, t2, core2, t3, core3, ln_g, ln_b, 
                 nc.sync.dma_start(out=t_raw[w, j][:], in_=t_rows[w][:, PAIR * j : PAIR * (j + 1), :])
 
         core_raw = [consts.tile([P, 2, PACK, DIM], BF16, name="core_raw%d" % w) for w in range(2)]
-        x_sb = consts.tile([P, TILES, K1], BF16)
+        x_sb = [consts.tile([P, X_BANK, K1], BF16, name="x_sb%d" % i) for i in range(TILES // X_BANK)]
+
+        def load_x(i):
+            nc.sync.dma_start(out=x_sb[i][:], in_=x_rows[:, X_BANK * i : X_BANK * (i + 1), :])
+
         for w in range(2):
             nc.sync.dma_start(out=core_raw[w][:].rearrange("p g (u e) d -> p g u e d", e=2), in_=core_rows[w])
-        load_t(0)
-        nc.sync.dma_start(out=x_sb[:], in_=x_rows)
-        for j in range(1, T_BUFS):
+        load_x(0)
+        for j in range(T_BUFS):
             load_t(j)
+            if 1 <= j - 1 < TILES // X_BANK:
+                load_x(j - 1)
 
         km1_sb = consts.tile([P, DIM], BF16)
         nc.scalar.dma_start(out=km1_sb[:], in_=km1.rearrange("i j d -> (i j) d"))
@@ -83,14 +89,20 @@ def tile_pinmodel_pa_t_kernel(tc, x, km1, b1, t2, core2, t3, core3, ln_g, ln_b, 
         nc.scalar.dma_start(out=gb_rows[0:PACK, :], in_=ln_g.rearrange("(t p) -> t p", p=P))
         nc.scalar.dma_start(out=gb_rows[PACK : 2 * PACK, :], in_=ln_b.rearrange("(t p) -> t p", p=P))
 
+        def regroup(copy, words, planes):
+            copy(
+                out=words.rearrange("p (c i) t -> p c t i", i=4),
+                in_=planes.rearrange("p t (c i) -> p c t i", i=4),
+            )
+
         ident_f32 = consts.tile([P, P], F32)
         make_identity(nc, ident_f32[:])
         ident_bf = consts.tile([P, P], BF16)
         make_identity(nc, ident_bf[:])
         ones = consts.tile([P, P], BF16)
         nc.vector.memset(ones[:], 1.0)
-        minus_half = consts.tile([P, PAIR], F32)
-        nc.vector.memset(minus_half[:], -0.5)
+        eps_col = consts.tile([P, 1], F32)
+        nc.vector.memset(eps_col[:], EPS)
 
         b1_ps = psum_o.tile([P, DIM], F32, tag="o")
         nc.tensor.matmul(b1_ps[:], lhsT=ones[:], rhs=vec_rows[:, 0:DIM], start=True, stop=True)
@@ -121,8 +133,8 @@ def tile_pinmodel_pa_t_kernel(tc, x, km1, b1, t2, core2, t3, core3, ln_g, ln_b, 
                 stage.tile([P, DIM, PACK], BF16, align_bytes=64, tag="core%d" % g, name="core_grouped%d_%d" % (w, g))
                 for g in range(2)
             ]
-            nc.vector.tensor_copy(out=core_grouped[0][:], in_=core_raw[w][:, 0].rearrange("p t d -> p d t"))
-            nc.scalar.copy(out=core_grouped[1][:], in_=core_raw[w][:, 1].rearrange("p t d -> p d t"))
+            regroup(nc.vector.tensor_copy, core_grouped[0][:], core_raw[w][:, 0])
+            regroup(nc.scalar.copy, core_grouped[1][:], core_raw[w][:, 1])
             if w == 0:
                 nc.vector.quantize_mx(
                     out=w_codes[:].bitcast(FP8X4), scales=w_scales[:], in_=w_grouped[:].rearrange("p o t -> p (o t)")
@@ -168,14 +180,15 @@ def tile_pinmodel_pa_t_kernel(tc, x, km1, b1, t2, core2, t3, core3, ln_g, ln_b, 
             )
             t_codes[j, m] = (codes, scales)
 
-        xT = consts.tile([P, TILES, P], BF16)
+        xT = [consts.tile([P, X_BANK, P], BF16, name="xT%d" % i) for i in range(TILES // X_BANK)]
         xkb_tiles = {}
 
         def plain_product(j, m):
             if not live(j):
                 return
             xk = psum_x.tile([P, DIM], F32, tag="x")
-            nc.tensor.matmul(xk[:], lhsT=xT[:, PAIR * j + m, :], rhs=km1_sb[:], start=True, stop=True)
+            i, n = divmod(PAIR * j + m, X_BANK)
+            nc.tensor.matmul(xk[:], lhsT=xT[i][:, n, :], rhs=km1_sb[:], start=True, stop=True)
             xkb = work.tile([P, DIM], F32)
             nc.vector.tensor_tensor(out=xkb[:], in0=xk[:], in1=b1_bc[:], op=ALU.add)
             xkb_tiles[j, m] = xkb
@@ -208,41 +221,37 @@ def tile_pinmodel_pa_t_kernel(tc, x, km1, b1, t2, core2, t3, core3, ln_g, ln_b, 
             o_tiles[j, m] = o
 
         neg_means = {}
-        sq_sums = {}
+        stds = {}
 
         def mean(j):
             if not live(j):
                 return
             neg_means[j] = small.tile([P, PAIR], F32, name="neg_mean")
-            nc.gpsimd.tensor_scalar(
-                out=neg_means[j][:], in0=o_sums[j][:], scalar1=-1.0 / DIM, scalar2=0.0, op0=ALU.mult, op1=ALU.add
-            )
+            nc.vector.tensor_scalar_mul(out=neg_means[j][:], in0=o_sums[j][:], scalar1=-1.0 / DIM)
 
         def deviation(j):
             if not live(j):
                 return
-            sq_sums[j] = small.tile([P, PAIR], F32, name="sq_sum")
+            sq_sum = small.tile([P, PAIR], F32)
             for m in range(PAIR):
                 squares = stage.tile([P, DIM], BF16)
                 nc.scalar.activation(
                     out=squares[:], in_=o_tiles[j, m][:], func=ACT.Square,
-                    bias=neg_means[j][:, m : m + 1], scale=1.0, accum_out=sq_sums[j][:, m : m + 1],
+                    bias=neg_means[j][:, m : m + 1], scale=1.0, accum_out=sq_sum[:, m : m + 1],
                 )
+            stds[j] = small.tile([P, PAIR], F32, name="std")
+            nc.scalar.activation(out=stds[j][:], in_=sq_sum[:], func=ACT.Sqrt, bias=eps_col[:], scale=1.0 / DIM)
 
         z_tiles = {}
 
         def normalise(j):
             if not live(j):
                 return
-            var_eps = small.tile([P, PAIR], F32)
-            nc.gpsimd.tensor_scalar(
-                out=var_eps[:], in0=sq_sums[j][:], scalar1=1.0 / DIM, scalar2=EPS, op0=ALU.mult, op1=ALU.add
-            )
             rstd = small.tile([P, PAIR], F32)
-            nc.gpsimd.tensor_tensor(out=rstd[:], in0=var_eps[:], in1=minus_half[:], op=ALU.pow)
+            nc.vector.reciprocal(out=rstd[:], in_=stds[j][:])
             for m in range(PAIR):
                 z = work.tile([P, DIM], F32)
-                nc.gpsimd.tensor_scalar(
+                nc.vector.tensor_scalar(
                     out=z[:], in0=o_tiles[j, m][:], scalar1=neg_means[j][:, m : m + 1], scalar2=rstd[:, m : m + 1],
                     op0=ALU.add, op1=ALU.mult,
                 )
@@ -253,23 +262,24 @@ def tile_pinmodel_pa_t_kernel(tc, x, km1, b1, t2, core2, t3, core3, ln_g, ln_b, 
         y_grouped = {}
         y_codes = {}
 
-        def transpose_z(j):
+        def transpose_z(j, half):
             if not live(j):
                 return
-            for half in range(2):
-                z_bank[j, half] = psum_z.tile([P, 2, PAIR, P], F32, tag="z", name="z_bank")
-                for tt in range(2):
-                    t = 2 * half + tt
-                    for m in range(PAIR):
-                        nc.tensor.transpose(z_bank[j, half][:, tt, m, :], z_tiles[j, m][:, P * t : P * (t + 1)], ident_f32[:])
+            z_bank[j, half] = psum_z.tile([P, 2, PAIR, P], F32, tag="z", name="z_bank")
+            for tt in range(2):
+                t = 2 * half + tt
+                for m in range(PAIR):
+                    nc.tensor.transpose(z_bank[j, half][:, tt, m, :], z_tiles[j, m][:, P * t : P * (t + 1)], ident_f32[:])
 
-        def scale_shift(j):
+        def scale_shift(j, half):
             if not live(j):
                 return
-            y_planes[j] = stage.tile([P, PACK, PAIR, P], BF16, name="y_planes")
-            for t in range(PACK):
+            if half == 0:
+                y_planes[j] = stage.tile([P, PACK, PAIR, P], BF16, name="y_planes")
+            for tt in range(2):
+                t = 2 * half + tt
                 nc.scalar.activation(
-                    out=y_planes[j][:, t, :, :], in_=z_bank[j, t // 2][:, t % 2, :, :], func=ACT.Identity,
+                    out=y_planes[j][:, t, :, :], in_=z_bank[j, half][:, tt, :, :], func=ACT.Identity,
                     scale=gb_col[:, t : t + 1], bias=gb_col[:, PACK + t : PACK + t + 1],
                 )
 
@@ -277,7 +287,11 @@ def tile_pinmodel_pa_t_kernel(tc, x, km1, b1, t2, core2, t3, core3, ln_g, ln_b, 
             if not live(j):
                 return
             y_grouped[j] = stage.tile([P, PAIR, P, PACK], BF16, align_bytes=64, name="y_grouped")
-            nc.vector.tensor_copy(out=y_grouped[j][:], in_=y_planes[j][:].rearrange("p t m r -> p m r t"))
+            regroup(
+                nc.vector.tensor_copy,
+                y_grouped[j][:].rearrange("p m r t -> p (m r) t"),
+                y_planes[j][:].rearrange("p t m r -> p t (m r)"),
+            )
 
         def quantise_y(j):
             if not live(j):
@@ -312,49 +326,33 @@ def tile_pinmodel_pa_t_kernel(tc, x, km1, b1, t2, core2, t3, core3, ln_g, ln_b, 
             )
             nc.sync.dma_start(out=out_rows[:, PAIR * j : PAIR * (j + 1), :], in_=result[:])
 
-        for m in range(PAIR):
-            for w in range(2):
-                transpose_t(0, m, w)
-                copy_t(0, m, w)
-        load_t(T_BUFS)
-        for m in range(PAIR):
-            quantise_t(0, m)
-        for i in range(TILES // 8):
-            x_bank = psum_t.tile([P, 8, P], BF16, tag="t")
-            for n in range(8 * i, 8 * i + 8):
-                nc.tensor.transpose(x_bank[:, n - 8 * i, :], x_sb[:, n, :], ident_bf[:])
-            nc.scalar.copy(out=xT[:, 8 * i : 8 * i + 8, :], in_=x_bank[:])
-        for m in range(PAIR):
-            for w in range(2):
-                transpose_t(1, m, w)
-                copy_t(1, m, w)
-        load_t(1 + T_BUFS)
-        for m in range(PAIR):
-            plain_product(0, m)
+        def transpose_x(i):
+            x_bank = psum_t.tile([P, X_BANK, P], BF16, tag="t")
+            for n in range(X_BANK):
+                nc.tensor.transpose(x_bank[:, n, :], x_sb[i][:, n, :], ident_bf[:])
+            nc.scalar.copy(out=xT[i][:], in_=x_bank[:])
 
-        for s in range(ROUNDS + 4):
+        rounds_per_bank = X_BANK // PAIR
+        for s in range(-3, ROUNDS + 3):
             quantise_t(s + 1, 0)
             regroup_y(s - 3)
             quantise_t(s + 1, 1)
             quantise_y(s - 3)
-
-            transpose_t(s + 2, 0, 0)
-            copy_t(s + 2, 0, 0)
-            transpose_t(s + 2, 0, 1)
-            copy_t(s + 2, 0, 1)
-            transpose_t(s + 2, 1, 0)
-            transpose_z(s - 2)
-            transpose_t(s + 2, 1, 1)
-            load_t(s + 2 + T_BUFS)
-            deviation(s - 1)
-            copy_t(s + 2, 1, 0)
-            copy_t(s + 2, 1, 1)
-            scale_shift(s - 2)
-
-            plain_product(s + 1, 0)
-            mx_products(s, 0)
-            plain_product(s + 1, 1)
-            normalise(s - 1)
-            mx_products(s, 1)
+            for m in range(PAIR):
+                for w in range(2):
+                    transpose_t(s + 2, m, w)
+                    copy_t(s + 2, m, w)
+                transpose_z(s - 2, m)
+                if m == 0:
+                    deviation(s - 1)
+                scale_shift(s - 2, m)
+                plain_product(s + 1, m)
+                mx_products(s, m)
+                if m == 0:
+                    normalise(s - 1)
+            if live(s + 2):
+                load_t(s + 2 + T_BUFS)
             mean(s)
             head(s - 3)
+            if (s + 3) % rounds_per_bank == 0 and live(s + 3):
+                transpose_x((s + 3) // rounds_per_bank)

@@ -40,8 +40,8 @@ def tile_pinmodel_pa_t_kernel(tc, x, km1, b1, t2, core2, t3, core3, ln_g, ln_b, 
         consts = stack.enter_context(tc.tile_pool(name="consts", bufs=1))
         t_pool = stack.enter_context(tc.tile_pool(name="t_pool", bufs=T_BUFS))
         stage = stack.enter_context(tc.tile_pool(name="stage", bufs=2))
-        grouped_pool = stack.enter_context(tc.tile_pool(name="grouped_pool", bufs=6))
-        tq = stack.enter_context(tc.tile_pool(name="tq", bufs=6))
+        grouped_pool = stack.enter_context(tc.tile_pool(name="grouped_pool", bufs=3))
+        tq = stack.enter_context(tc.tile_pool(name="tq", bufs=3))
         work = stack.enter_context(tc.tile_pool(name="work", bufs=6))
         small = stack.enter_context(tc.tile_pool(name="small", bufs=4))
         yq = stack.enter_context(tc.tile_pool(name="yq", bufs=3))
@@ -161,24 +161,24 @@ def tile_pinmodel_pa_t_kernel(tc, x, km1, b1, t2, core2, t3, core3, ln_g, ln_b, 
         def copy_t(j, m, w):
             if not live(j):
                 return
-            if w == 0:
-                t_grouped[j, m] = grouped_pool.tile([P, 2, 2, P, PACK], BF16, align_bytes=64, name="t_grouped")
+            if m == 0 and w == 0:
+                t_grouped[j] = grouped_pool.tile([P, PAIR, 2, 2, P, PACK], BF16, align_bytes=64, name="t_grouped")
             nc.scalar.copy(
-                out=t_grouped[j, m][:].bitcast(F32)[:, w],
+                out=t_grouped[j][:].bitcast(F32)[:, m, w],
                 in_=t_bank[j, m, w][:].rearrange("p (g u) r -> p g r u", u=2),
             )
 
-        def quantise_t(j, m):
+        def quantise_t(j):
             if not live(j):
                 return
-            codes = tq.tile([P, PASSES, P], U32, align_bytes=64)
-            scales = tq.tile([P, PASSES, P], U8, align_bytes=64)
+            codes = tq.tile([P, PAIR, PASSES, P], U32, align_bytes=64)
+            scales = tq.tile([P, PAIR, PASSES, P], U8, align_bytes=64)
             nc.vector.quantize_mx(
-                out=codes[:].rearrange("p c r -> p (c r)").bitcast(FP8X4),
-                scales=scales[:].rearrange("p c r -> p (c r)"),
-                in_=t_grouped[j, m][:].rearrange("p w g r t -> p (w g r t)"),
+                out=codes[:].rearrange("p m c r -> p (m c r)").bitcast(FP8X4),
+                scales=scales[:].rearrange("p m c r -> p (m c r)"),
+                in_=t_grouped[j][:].rearrange("p m w g r t -> p (m w g r t)"),
             )
-            t_codes[j, m] = (codes, scales)
+            t_codes[j] = (codes, scales)
 
         xT = [consts.tile([P, X_BANK, P], BF16, name="xT%d" % i) for i in range(TILES // X_BANK)]
         xkb_tiles = {}
@@ -201,13 +201,13 @@ def tile_pinmodel_pa_t_kernel(tc, x, km1, b1, t2, core2, t3, core3, ln_g, ln_b, 
                 return
             if m == 0:
                 o_sums[j] = small.tile([P, PAIR], F32, name="o_sum")
-            codes, scales = t_codes[j, m]
+            codes, scales = t_codes[j]
             acc = psum_o.tile([P, DIM], F32, tag="o")
             for c in range(PASSES):
                 nc.tensor.matmul_mx(
                     out=acc[:],
-                    lhsT=codes[:, c, :].bitcast(FP8X4),
-                    lhsT_scale=scales[:, c, :],
+                    lhsT=codes[:, m, c, :].bitcast(FP8X4),
+                    lhsT_scale=scales[:, m, c, :],
                     rhs=core_codes[:, c, :].bitcast(FP8X4),
                     rhs_scale=core_scales[:, c, :],
                     start=(c == 0),
@@ -221,17 +221,13 @@ def tile_pinmodel_pa_t_kernel(tc, x, km1, b1, t2, core2, t3, core3, ln_g, ln_b, 
             o_tiles[j, m] = o
 
         neg_means = {}
-        stds = {}
+        rstds = {}
 
-        def mean(j):
+        def statistics(j):
             if not live(j):
                 return
             neg_means[j] = small.tile([P, PAIR], F32, name="neg_mean")
-            nc.vector.tensor_scalar_mul(out=neg_means[j][:], in0=o_sums[j][:], scalar1=-1.0 / DIM)
-
-        def deviation(j):
-            if not live(j):
-                return
+            nc.scalar.mul(out=neg_means[j][:], in_=o_sums[j][:], mul=-1.0 / DIM)
             sq_sum = small.tile([P, PAIR], F32)
             for m in range(PAIR):
                 squares = stage.tile([P, DIM], BF16)
@@ -239,23 +235,22 @@ def tile_pinmodel_pa_t_kernel(tc, x, km1, b1, t2, core2, t3, core3, ln_g, ln_b, 
                     out=squares[:], in_=o_tiles[j, m][:], func=ACT.Square,
                     bias=neg_means[j][:, m : m + 1], scale=1.0, accum_out=sq_sum[:, m : m + 1],
                 )
-            stds[j] = small.tile([P, PAIR], F32, name="std")
-            nc.scalar.activation(out=stds[j][:], in_=sq_sum[:], func=ACT.Sqrt, bias=eps_col[:], scale=1.0 / DIM)
+            rstds[j] = small.tile([P, PAIR], F32, name="rstd")
+            nc.scalar.activation(
+                out=rstds[j][:], in_=sq_sum[:], func=ACT.Abs_reciprocal_sqrt, bias=eps_col[:], scale=1.0 / DIM
+            )
 
         z_tiles = {}
 
-        def normalise(j):
+        def normalise(j, m):
             if not live(j):
                 return
-            rstd = small.tile([P, PAIR], F32)
-            nc.vector.reciprocal(out=rstd[:], in_=stds[j][:])
-            for m in range(PAIR):
-                z = work.tile([P, DIM], F32)
-                nc.vector.tensor_scalar(
-                    out=z[:], in0=o_tiles[j, m][:], scalar1=neg_means[j][:, m : m + 1], scalar2=rstd[:, m : m + 1],
-                    op0=ALU.add, op1=ALU.mult,
-                )
-                z_tiles[j, m] = z
+            z = work.tile([P, DIM], F32)
+            nc.vector.tensor_scalar(
+                out=z[:], in0=o_tiles[j, m][:], scalar1=neg_means[j][:, m : m + 1], scalar2=rstds[j][:, m : m + 1],
+                op0=ALU.add, op1=ALU.mult,
+            )
+            z_tiles[j, m] = z
 
         z_bank = {}
         y_planes = {}
@@ -334,9 +329,8 @@ def tile_pinmodel_pa_t_kernel(tc, x, km1, b1, t2, core2, t3, core3, ln_g, ln_b, 
 
         rounds_per_bank = X_BANK // PAIR
         for s in range(-3, ROUNDS + 3):
-            quantise_t(s + 1, 0)
             regroup_y(s - 3)
-            quantise_t(s + 1, 1)
+            quantise_t(s + 1)
             quantise_y(s - 3)
             for m in range(PAIR):
                 for w in range(2):
@@ -344,15 +338,16 @@ def tile_pinmodel_pa_t_kernel(tc, x, km1, b1, t2, core2, t3, core3, ln_g, ln_b, 
                     copy_t(s + 2, m, w)
                 transpose_z(s - 2, m)
                 if m == 0:
-                    deviation(s - 1)
+                    statistics(s - 1)
                 scale_shift(s - 2, m)
                 plain_product(s + 1, m)
+                if m == 1:
+                    normalise(s - 1, 1)
                 mx_products(s, m)
                 if m == 0:
-                    normalise(s - 1)
+                    normalise(s - 1, 0)
             if live(s + 2):
                 load_t(s + 2 + T_BUFS)
-            mean(s)
             head(s - 3)
             if (s + 3) % rounds_per_bank == 0 and live(s + 3):
                 transpose_x((s + 3) // rounds_per_bank)

@@ -16,9 +16,7 @@ PACK = 4
 B, K1, KR, DIM, OUT = 4096, 128, 1024, 512, 128
 EPS = 1e-5
 TILES = B // P
-PAIR = 2
-ROUNDS = TILES // PAIR
-T_BUFS = 8
+T_BUFS = 16
 X_BANK = 8
 PASSES = 2 * KR // (P * PACK)
 
@@ -40,27 +38,23 @@ def tile_pinmodel_pa_t_kernel(tc, x, km1, b1, t2, core2, t3, core3, ln_g, ln_b, 
         consts = stack.enter_context(tc.tile_pool(name="consts", bufs=1))
         t_pool = stack.enter_context(tc.tile_pool(name="t_pool", bufs=T_BUFS))
         stage = stack.enter_context(tc.tile_pool(name="stage", bufs=2))
-        grouped_pool = stack.enter_context(tc.tile_pool(name="grouped_pool", bufs=3))
-        tq = stack.enter_context(tc.tile_pool(name="tq", bufs=3))
-        work = stack.enter_context(tc.tile_pool(name="work", bufs=6))
-        small = stack.enter_context(tc.tile_pool(name="small", bufs=4))
-        yq = stack.enter_context(tc.tile_pool(name="yq", bufs=3))
+        work = stack.enter_context(tc.tile_pool(name="work", bufs=4))
         psum_t = stack.enter_context(tc.psum_pool(name="psum_t", bufs=3))
         psum_z = stack.enter_context(tc.psum_pool(name="psum_z", bufs=2))
         psum_o = stack.enter_context(tc.psum_pool(name="psum_o", bufs=2))
         psum_x = stack.enter_context(tc.psum_pool(name="psum_x", bufs=1))
 
-        def live(j):
-            return 0 <= j < ROUNDS
+        def live(n):
+            return 0 <= n < TILES
 
         t_raw = {}
 
-        def load_t(j):
-            if not live(j):
+        def load_t(n):
+            if not live(n):
                 return
             for w in range(2):
-                t_raw[w, j] = t_pool.tile([P, PAIR, KR], BF16, tag="t%d" % w, name="t%d_%d" % (w, j))
-                nc.sync.dma_start(out=t_raw[w, j][:], in_=t_rows[w][:, PAIR * j : PAIR * (j + 1), :])
+                t_raw[w, n] = t_pool.tile([P, KR], BF16, tag="t%d" % w, name="t%d_%d" % (w, n))
+                nc.sync.dma_start(out=t_raw[w, n][:], in_=t_rows[w][:, n, :])
 
         core_raw = [consts.tile([P, 2, PACK, DIM], BF16, name="core_raw%d" % w) for w in range(2)]
         x_sb = [consts.tile([P, X_BANK, K1], BF16, name="x_sb%d" % i) for i in range(TILES // X_BANK)]
@@ -70,11 +64,11 @@ def tile_pinmodel_pa_t_kernel(tc, x, km1, b1, t2, core2, t3, core3, ln_g, ln_b, 
 
         for w in range(2):
             nc.sync.dma_start(out=core_raw[w][:].rearrange("p g (u e) d -> p g u e d", e=2), in_=core_rows[w])
-        load_x(0)
-        for j in range(T_BUFS):
-            load_t(j)
-            if 1 <= j - 1 < TILES // X_BANK:
-                load_x(j - 1)
+        t_per_x = T_BUFS * X_BANK // TILES
+        for n in range(T_BUFS):
+            if n % t_per_x == 0:
+                load_x(n // t_per_x)
+            load_t(n)
 
         km1_sb = consts.tile([P, DIM], BF16)
         nc.scalar.dma_start(out=km1_sb[:], in_=km1.rearrange("i j d -> (i j) d"))
@@ -146,180 +140,7 @@ def tile_pinmodel_pa_t_kernel(tc, x, km1, b1, t2, core2, t3, core3, ln_g, ln_b, 
                     in_=core_grouped[g][:].rearrange("p d t -> p (d t)"),
                 )
 
-        t_bank = {}
-        t_grouped = {}
-        t_codes = {}
-
-        def transpose_t(j, m, w):
-            if not live(j):
-                return
-            words = t_raw[w, j][:].bitcast(F32)
-            t_bank[j, m, w] = psum_t.tile([P, 4, P], F32, tag="t", name="t_bank")
-            for q in range(4):
-                nc.tensor.transpose(t_bank[j, m, w][:, q, :], words[:, m, P * q : P * (q + 1)], ident_f32[:])
-
-        def copy_t(j, m, w):
-            if not live(j):
-                return
-            if m == 0 and w == 0:
-                t_grouped[j] = grouped_pool.tile([P, PAIR, 2, 2, P, PACK], BF16, align_bytes=64, name="t_grouped")
-            nc.scalar.copy(
-                out=t_grouped[j][:].bitcast(F32)[:, m, w],
-                in_=t_bank[j, m, w][:].rearrange("p (g u) r -> p g r u", u=2),
-            )
-
-        def quantise_t(j):
-            if not live(j):
-                return
-            codes = tq.tile([P, PAIR, PASSES, P], U32, align_bytes=64)
-            scales = tq.tile([P, PAIR, PASSES, P], U8, align_bytes=64)
-            nc.vector.quantize_mx(
-                out=codes[:].rearrange("p m c r -> p (m c r)").bitcast(FP8X4),
-                scales=scales[:].rearrange("p m c r -> p (m c r)"),
-                in_=t_grouped[j][:].rearrange("p m w g r t -> p (m w g r t)"),
-            )
-            t_codes[j] = (codes, scales)
-
         xT = [consts.tile([P, X_BANK, P], BF16, name="xT%d" % i) for i in range(TILES // X_BANK)]
-        xkb_tiles = {}
-
-        def plain_product(j, m):
-            if not live(j):
-                return
-            xk = psum_x.tile([P, DIM], F32, tag="x")
-            i, n = divmod(PAIR * j + m, X_BANK)
-            nc.tensor.matmul(xk[:], lhsT=xT[i][:, n, :], rhs=km1_sb[:], start=True, stop=True)
-            xkb = work.tile([P, DIM], F32)
-            nc.vector.tensor_tensor(out=xkb[:], in0=xk[:], in1=b1_bc[:], op=ALU.add)
-            xkb_tiles[j, m] = xkb
-
-        o_tiles = {}
-        o_sums = {}
-
-        def mx_products(j, m):
-            if not live(j):
-                return
-            if m == 0:
-                o_sums[j] = small.tile([P, PAIR], F32, name="o_sum")
-            codes, scales = t_codes[j]
-            acc = psum_o.tile([P, DIM], F32, tag="o")
-            for c in range(PASSES):
-                nc.tensor.matmul_mx(
-                    out=acc[:],
-                    lhsT=codes[:, m, c, :].bitcast(FP8X4),
-                    lhsT_scale=scales[:, m, c, :],
-                    rhs=core_codes[:, c, :].bitcast(FP8X4),
-                    rhs_scale=core_scales[:, c, :],
-                    start=(c == 0),
-                    stop=(c == PASSES - 1),
-                )
-            o = work.tile([P, DIM], F32)
-            nc.vector.scalar_tensor_tensor(
-                out=o[:], in0=acc[:], scalar=0.0, in1=xkb_tiles[j, m][:], op0=ALU.add, op1=ALU.add,
-                accum_out=o_sums[j][:, m : m + 1],
-            )
-            o_tiles[j, m] = o
-
-        neg_means = {}
-        rstds = {}
-
-        def statistics(j):
-            if not live(j):
-                return
-            neg_means[j] = small.tile([P, PAIR], F32, name="neg_mean")
-            nc.scalar.mul(out=neg_means[j][:], in_=o_sums[j][:], mul=-1.0 / DIM)
-            sq_sum = small.tile([P, PAIR], F32)
-            for m in range(PAIR):
-                squares = stage.tile([P, DIM], BF16)
-                nc.scalar.activation(
-                    out=squares[:], in_=o_tiles[j, m][:], func=ACT.Square,
-                    bias=neg_means[j][:, m : m + 1], scale=1.0, accum_out=sq_sum[:, m : m + 1],
-                )
-            rstds[j] = small.tile([P, PAIR], F32, name="rstd")
-            nc.scalar.activation(
-                out=rstds[j][:], in_=sq_sum[:], func=ACT.Abs_reciprocal_sqrt, bias=eps_col[:], scale=1.0 / DIM
-            )
-
-        z_tiles = {}
-
-        def normalise(j, m):
-            if not live(j):
-                return
-            z = work.tile([P, DIM], F32)
-            nc.vector.tensor_scalar(
-                out=z[:], in0=o_tiles[j, m][:], scalar1=neg_means[j][:, m : m + 1], scalar2=rstds[j][:, m : m + 1],
-                op0=ALU.add, op1=ALU.mult,
-            )
-            z_tiles[j, m] = z
-
-        z_bank = {}
-        y_planes = {}
-        y_grouped = {}
-        y_codes = {}
-
-        def transpose_z(j, half):
-            if not live(j):
-                return
-            z_bank[j, half] = psum_z.tile([P, 2, PAIR, P], F32, tag="z", name="z_bank")
-            for tt in range(2):
-                t = 2 * half + tt
-                for m in range(PAIR):
-                    nc.tensor.transpose(z_bank[j, half][:, tt, m, :], z_tiles[j, m][:, P * t : P * (t + 1)], ident_f32[:])
-
-        def scale_shift(j, half):
-            if not live(j):
-                return
-            if half == 0:
-                y_planes[j] = stage.tile([P, PACK, PAIR, P], BF16, name="y_planes")
-            for tt in range(2):
-                t = 2 * half + tt
-                nc.scalar.activation(
-                    out=y_planes[j][:, t, :, :], in_=z_bank[j, half][:, tt, :, :], func=ACT.Identity,
-                    scale=gb_col[:, t : t + 1], bias=gb_col[:, PACK + t : PACK + t + 1],
-                )
-
-        def regroup_y(j):
-            if not live(j):
-                return
-            y_grouped[j] = stage.tile([P, PAIR, P, PACK], BF16, align_bytes=64, name="y_grouped")
-            regroup(
-                nc.vector.tensor_copy,
-                y_grouped[j][:].rearrange("p m r t -> p (m r) t"),
-                y_planes[j][:].rearrange("p t m r -> p t (m r)"),
-            )
-
-        def quantise_y(j):
-            if not live(j):
-                return
-            codes = yq.tile([P, PAIR, P], U32, align_bytes=64, name="y_code")
-            scales = yq.tile([P, PAIR, P], U8, align_bytes=64, name="y_scale")
-            nc.vector.quantize_mx(
-                out=codes[:].rearrange("p m r -> p (m r)").bitcast(FP8X4),
-                scales=scales[:].rearrange("p m r -> p (m r)"),
-                in_=y_grouped[j][:].rearrange("p m r t -> p (m r t)"),
-            )
-            y_codes[j] = (codes, scales)
-
-        def head(j):
-            if not live(j):
-                return
-            codes, scales = y_codes[j]
-            fin = psum_x.tile([P, PAIR, OUT], F32, tag="x")
-            for m in range(PAIR):
-                nc.tensor.matmul_mx(
-                    out=fin[:, m, :],
-                    lhsT=codes[:, m, :].bitcast(FP8X4),
-                    lhsT_scale=scales[:, m, :],
-                    rhs=w_codes[:].bitcast(FP8X4),
-                    rhs_scale=w_scales[:],
-                    start=True,
-                    stop=True,
-                )
-            result = yq.tile([P, PAIR, OUT], F32)
-            nc.vector.tensor_tensor(
-                out=result[:], in0=fin[:], in1=fcb_bc[:].unsqueeze(1).to_broadcast([P, PAIR, OUT]), op=ALU.add
-            )
-            nc.sync.dma_start(out=out_rows[:, PAIR * j : PAIR * (j + 1), :], in_=result[:])
 
         def transpose_x(i):
             x_bank = psum_t.tile([P, X_BANK, P], BF16, tag="t")
@@ -327,27 +148,189 @@ def tile_pinmodel_pa_t_kernel(tc, x, km1, b1, t2, core2, t3, core3, ln_g, ln_b, 
                 nc.tensor.transpose(x_bank[:, n, :], x_sb[i][:, n, :], ident_bf[:])
             nc.scalar.copy(out=xT[i][:], in_=x_bank[:])
 
-        rounds_per_bank = X_BANK // PAIR
-        for s in range(-3, ROUNDS + 3):
-            regroup_y(s - 3)
-            quantise_t(s + 1)
-            quantise_y(s - 3)
-            for m in range(PAIR):
-                for w in range(2):
-                    transpose_t(s + 2, m, w)
-                    copy_t(s + 2, m, w)
-                transpose_z(s - 2, m)
-                if m == 0:
-                    statistics(s - 1)
-                scale_shift(s - 2, m)
-                plain_product(s + 1, m)
-                if m == 1:
-                    normalise(s - 1, 1)
-                mx_products(s, m)
-                if m == 0:
-                    normalise(s - 1, 0)
-            if live(s + 2):
-                load_t(s + 2 + T_BUFS)
-            head(s - 3)
-            if (s + 3) % rounds_per_bank == 0 and live(s + 3):
-                transpose_x((s + 3) // rounds_per_bank)
+        t_grouped = {}
+        t_codes = {}
+
+        def transpose_t(n):
+            if not live(n):
+                return
+            t_grouped[n] = work.tile([P, 2, 2, P, PACK], BF16, align_bytes=64, name="t_grouped")
+            for w in range(2):
+                words = t_raw[w, n][:].bitcast(F32)
+                t_bank = psum_t.tile([P, 4, P], F32, tag="t")
+                for q in range(4):
+                    nc.tensor.transpose(t_bank[:, q, :], words[:, P * q : P * (q + 1)], ident_f32[:])
+                nc.scalar.copy(
+                    out=t_grouped[n][:].bitcast(F32)[:, w],
+                    in_=t_bank[:].rearrange("p (g u) r -> p g r u", u=2),
+                )
+            load_t(n + T_BUFS)
+
+        def quantise_t(n):
+            if not live(n):
+                return
+            codes = work.tile([P, PASSES, P], U32, align_bytes=64, name="t_code")
+            scales = work.tile([P, PASSES, P], U8, align_bytes=64, name="t_scale")
+            nc.vector.quantize_mx(
+                out=codes[:].rearrange("p c r -> p (c r)").bitcast(FP8X4),
+                scales=scales[:].rearrange("p c r -> p (c r)"),
+                in_=t_grouped[n][:].rearrange("p w g r t -> p (w g r t)"),
+            )
+            t_codes[n] = (codes, scales)
+
+        xkb_tiles = {}
+
+        def plain_product(n):
+            if not live(n):
+                return
+            xk = psum_x.tile([P, DIM], F32, tag="x")
+            nc.tensor.matmul(xk[:], lhsT=xT[n // X_BANK][:, n % X_BANK, :], rhs=km1_sb[:], start=True, stop=True)
+            xkb_tiles[n] = work.tile([P, DIM], F32, name="xkb")
+            nc.vector.tensor_tensor(out=xkb_tiles[n][:], in0=xk[:], in1=b1_bc[:], op=ALU.add)
+
+        acc_banks = {}
+
+        def mx_products(n):
+            if not live(n):
+                return
+            codes, scales = t_codes[n]
+            acc_banks[n] = psum_o.tile([P, DIM], F32, tag="o", name="acc")
+            for c in range(PASSES):
+                nc.tensor.matmul_mx(
+                    out=acc_banks[n][:],
+                    lhsT=codes[:, c, :].bitcast(FP8X4),
+                    lhsT_scale=scales[:, c, :],
+                    rhs=core_codes[:, c, :].bitcast(FP8X4),
+                    rhs_scale=core_scales[:, c, :],
+                    start=(c == 0),
+                    stop=(c == PASSES - 1),
+                )
+
+        o_tiles = {}
+        o_sums = {}
+
+        def add_terms(n):
+            if not live(n):
+                return
+            o_tiles[n] = work.tile([P, DIM], F32, name="o")
+            o_sums[n] = work.tile([P, 1], F32, name="o_sum")
+            nc.vector.scalar_tensor_tensor(
+                out=o_tiles[n][:], in0=acc_banks[n][:], scalar=0.0, in1=xkb_tiles[n][:], op0=ALU.add, op1=ALU.add,
+                accum_out=o_sums[n][:],
+            )
+
+        neg_means = {}
+        sq_sums = {}
+        rstds = {}
+
+        def mean(n):
+            if not live(n):
+                return
+            neg_means[n] = work.tile([P, 1], F32, name="neg_mean")
+            nc.scalar.mul(out=neg_means[n][:], in_=o_sums[n][:], mul=-1.0 / DIM)
+
+        def squares(n):
+            if not live(n):
+                return
+            squared = stage.tile([P, DIM], BF16)
+            sq_sums[n] = work.tile([P, 1], F32, name="sq_sum")
+            nc.scalar.activation(
+                out=squared[:], in_=o_tiles[n][:], func=ACT.Square, bias=neg_means[n][:], scale=1.0,
+                accum_out=sq_sums[n][:],
+            )
+
+        def inverse_deviation(n):
+            if not live(n):
+                return
+            rstds[n] = work.tile([P, 1], F32, name="rstd")
+            nc.scalar.activation(
+                out=rstds[n][:], in_=sq_sums[n][:], func=ACT.Abs_reciprocal_sqrt, bias=eps_col[:], scale=1.0 / DIM
+            )
+
+        z_tiles = {}
+
+        def normalise(n):
+            if not live(n):
+                return
+            z_tiles[n] = work.tile([P, DIM], F32, name="z")
+            nc.vector.tensor_scalar(
+                out=z_tiles[n][:], in0=o_tiles[n][:], scalar1=neg_means[n][:], scalar2=rstds[n][:],
+                op0=ALU.add, op1=ALU.mult,
+            )
+
+        z_banks = {}
+        y_planes = {}
+        y_grouped = {}
+        y_codes = {}
+
+        def transpose_z(n):
+            if not live(n):
+                return
+            z_banks[n] = psum_z.tile([P, PACK, P], F32, tag="z", name="z_bank")
+            for t in range(PACK):
+                nc.tensor.transpose(z_banks[n][:, t, :], z_tiles[n][:, P * t : P * (t + 1)], ident_f32[:])
+
+        def scale_shift(n, t):
+            if not live(n):
+                return
+            if t == 0:
+                y_planes[n] = work.tile([P, PACK, P], BF16, name="y_planes")
+            nc.scalar.activation(
+                out=y_planes[n][:, t, :], in_=z_banks[n][:, t, :], func=ACT.Identity,
+                scale=gb_col[:, t : t + 1], bias=gb_col[:, PACK + t : PACK + t + 1],
+            )
+
+        def regroup_y(n):
+            if not live(n):
+                return
+            y_grouped[n] = work.tile([P, P, PACK], BF16, align_bytes=64, name="y_grouped")
+            regroup(nc.vector.tensor_copy, y_grouped[n][:], y_planes[n][:])
+
+        def quantise_y(n):
+            if not live(n):
+                return
+            codes = work.tile([P, P], U32, align_bytes=64, name="y_code")
+            scales = work.tile([P, P], U8, align_bytes=64, name="y_scale")
+            nc.vector.quantize_mx(
+                out=codes[:].bitcast(FP8X4), scales=scales[:], in_=y_grouped[n][:].rearrange("p r t -> p (r t)")
+            )
+            y_codes[n] = (codes, scales)
+
+        def head(n):
+            if not live(n):
+                return
+            codes, scales = y_codes[n]
+            fin = psum_x.tile([P, OUT], F32, tag="x")
+            nc.tensor.matmul_mx(
+                out=fin[:],
+                lhsT=codes[:].bitcast(FP8X4),
+                lhsT_scale=scales[:],
+                rhs=w_codes[:].bitcast(FP8X4),
+                rhs_scale=w_scales[:],
+                start=True,
+                stop=True,
+            )
+            result = work.tile([P, OUT], F32)
+            nc.vector.tensor_tensor(out=result[:], in0=fin[:], in1=fcb_bc[:], op=ALU.add)
+            nc.sync.dma_start(out=out_rows[:, n, :], in_=result[:])
+
+        for s in range(-4, TILES + 6):
+            quantise_t(s + 2)
+            regroup_y(s - 5)
+            mean(s - 2)
+            transpose_t(s + 3)
+            transpose_z(s - 4)
+            squares(s - 2)
+            scale_shift(s - 4, 0)
+            scale_shift(s - 4, 1)
+            inverse_deviation(s - 2)
+            scale_shift(s - 4, 2)
+            scale_shift(s - 4, 3)
+            plain_product(s + 1)
+            normalise(s - 3)
+            mx_products(s)
+            add_terms(s - 1)
+            head(s - 6)
+            quantise_y(s - 5)
+            if (s + 4) % X_BANK == 0 and live(s + 4):
+                transpose_x((s + 4) // X_BANK)

@@ -100,25 +100,15 @@ def tile_pinmodel_pa_t_kernel(tc, x, km1, b1, t2, core2, t3, core3, ln_g, ln_b, 
 
         b1_ps = psum_o.tile([P, DIM], F32, tag="o")
         nc.tensor.matmul(b1_ps[:], lhsT=ones[:], rhs=vec_rows[:, 0:DIM], start=True, stop=True)
-        b1_bc = consts.tile([P, DIM], F32)
-        nc.vector.tensor_copy(out=b1_bc[:], in_=b1_ps[:])
         fcb_ps = psum_o.tile([P, OUT], F32, tag="o")
         nc.tensor.matmul(fcb_ps[:], lhsT=ones[:], rhs=vec_rows[:, DIM : DIM + OUT], start=True, stop=True)
-        fcb_bc = consts.tile([P, OUT], F32)
-        nc.vector.tensor_copy(out=fcb_bc[:], in_=fcb_ps[:])
 
         gb_ps = psum_z.tile([P, P], BF16, tag="z")
         nc.tensor.transpose(gb_ps[:], gb_rows[:], ident_bf[:])
-        gb_col = consts.tile([P, 2 * PACK], F32)
-        nc.vector.tensor_copy(out=gb_col[:], in_=gb_ps[:, 0 : 2 * PACK])
 
         w_ps = psum_z.tile([P, PACK, OUT], BF16, tag="z")
         for t in range(PACK):
             nc.tensor.transpose(w_ps[:, t, :], fcw_sb[:, P * t : P * (t + 1)], ident_bf[:])
-        w_grouped = consts.tile([P, OUT, PACK], BF16, align_bytes=64)
-        nc.vector.tensor_copy(out=w_grouped[:], in_=w_ps[:].rearrange("p t o -> p o t"))
-        w_codes = consts.tile([P, OUT], U32, align_bytes=64)
-        w_scales = consts.tile([P, OUT], U8, align_bytes=64)
 
         core_codes = consts.tile([P, PASSES, DIM], U32, align_bytes=64)
         core_scales = consts.tile([P, PASSES, DIM], U8, align_bytes=64)
@@ -129,16 +119,26 @@ def tile_pinmodel_pa_t_kernel(tc, x, km1, b1, t2, core2, t3, core3, ln_g, ln_b, 
             ]
             regroup(nc.vector.tensor_copy, core_grouped[0][:], core_raw[w][:, 0])
             regroup(nc.scalar.copy, core_grouped[1][:], core_raw[w][:, 1])
-            if w == 0:
-                nc.vector.quantize_mx(
-                    out=w_codes[:].bitcast(FP8X4), scales=w_scales[:], in_=w_grouped[:].rearrange("p o t -> p (o t)")
-                )
             for g in range(2):
                 nc.vector.quantize_mx(
                     out=core_codes[:, 2 * w + g, :].bitcast(FP8X4),
                     scales=core_scales[:, 2 * w + g, :],
                     in_=core_grouped[g][:].rearrange("p d t -> p (d t)"),
                 )
+
+        b1_bc = consts.tile([P, DIM], F32)
+        nc.vector.tensor_copy(out=b1_bc[:], in_=b1_ps[:])
+        w_grouped = consts.tile([P, OUT, PACK], BF16, align_bytes=64)
+        nc.vector.tensor_copy(out=w_grouped[:], in_=w_ps[:].rearrange("p t o -> p o t"))
+        fcb_bc = consts.tile([P, OUT], F32)
+        nc.vector.tensor_copy(out=fcb_bc[:], in_=fcb_ps[:])
+        gb_col = consts.tile([P, 2 * PACK], F32)
+        nc.vector.tensor_copy(out=gb_col[:], in_=gb_ps[:, 0 : 2 * PACK])
+        w_codes = consts.tile([P, OUT], U32, align_bytes=64)
+        w_scales = consts.tile([P, OUT], U8, align_bytes=64)
+        nc.vector.quantize_mx(
+            out=w_codes[:].bitcast(FP8X4), scales=w_scales[:], in_=w_grouped[:].rearrange("p o t -> p (o t)")
+        )
 
         xT = [consts.tile([P, X_BANK, P], BF16, name="xT%d" % i) for i in range(TILES // X_BANK)]
 
@@ -300,7 +300,7 @@ def tile_pinmodel_pa_t_kernel(tc, x, km1, b1, t2, core2, t3, core3, ln_g, ln_b, 
             if not live(n):
                 return
             codes, scales = y_codes[n]
-            fin = psum_x.tile([P, OUT], F32, tag="x")
+            fin = psum_t.tile([P, OUT], F32, tag="t")
             nc.tensor.matmul_mx(
                 out=fin[:],
                 lhsT=codes[:].bitcast(FP8X4),
@@ -315,10 +315,12 @@ def tile_pinmodel_pa_t_kernel(tc, x, km1, b1, t2, core2, t3, core3, ln_g, ln_b, 
             nc.sync.dma_start(out=out_rows[:, n, :], in_=result[:])
 
         for s in range(-4, TILES + 6):
-            quantise_t(s + 2)
+            quantise_t(s)
+            add_terms(s - 1)
+            normalise(s - 3)
             regroup_y(s - 5)
             mean(s - 2)
-            transpose_t(s + 3)
+            transpose_t(s + 2)
             transpose_z(s - 4)
             squares(s - 2)
             scale_shift(s - 4, 0)
@@ -327,10 +329,8 @@ def tile_pinmodel_pa_t_kernel(tc, x, km1, b1, t2, core2, t3, core3, ln_g, ln_b, 
             scale_shift(s - 4, 2)
             scale_shift(s - 4, 3)
             plain_product(s + 1)
-            normalise(s - 3)
-            mx_products(s)
-            add_terms(s - 1)
-            head(s - 6)
             quantise_y(s - 5)
+            head(s - 6)
+            mx_products(s)
             if (s + 4) % X_BANK == 0 and live(s + 4):
                 transpose_x((s + 4) // X_BANK)

@@ -18,6 +18,7 @@ EPS = 1e-5
 TILES = B // P
 T_BUFS = 16
 X_BANK = 8
+PAIR = 2
 PASSES = 2 * KR // (P * PACK)
 
 FLOPS = 2 * B * DIM * (K1 + 2 * KR) + 2 * B * DIM * OUT
@@ -74,10 +75,13 @@ def tile_pinmodel_pa_t_kernel(tc, x, km1, b1, t2, core2, t3, core3, ln_g, ln_b, 
         nc.scalar.dma_start(out=km1_sb[:], in_=km1.rearrange("i j d -> (i j) d"))
         fcw_sb = consts.tile([P, DIM], BF16)
         nc.scalar.dma_start(out=fcw_sb[:], in_=fc_w)
-        vec_rows = consts.tile([P, DIM + OUT], BF16)
+        vec_rows = consts.tile([P, DIM + PAIR * OUT], BF16)
         nc.vector.memset(vec_rows[:], 0.0)
         nc.scalar.dma_start(out=vec_rows[0:1, 0:DIM], in_=b1.rearrange("(o n) -> o n", o=1))
-        nc.scalar.dma_start(out=vec_rows[0:1, DIM : DIM + OUT], in_=fc_b.rearrange("(o n) -> o n", o=1))
+        for i in range(PAIR):
+            nc.scalar.dma_start(
+                out=vec_rows[0:1, DIM + OUT * i : DIM + OUT * (i + 1)], in_=fc_b.rearrange("(o n) -> o n", o=1)
+            )
         gb_rows = consts.tile([P, P], BF16)
         nc.vector.memset(gb_rows[:], 0.0)
         nc.scalar.dma_start(out=gb_rows[0:PACK, :], in_=ln_g.rearrange("(t p) -> t p", p=P))
@@ -100,8 +104,8 @@ def tile_pinmodel_pa_t_kernel(tc, x, km1, b1, t2, core2, t3, core3, ln_g, ln_b, 
 
         b1_ps = psum_o.tile([P, DIM], F32, tag="o")
         nc.tensor.matmul(b1_ps[:], lhsT=ones[:], rhs=vec_rows[:, 0:DIM], start=True, stop=True)
-        fcb_ps = psum_o.tile([P, OUT], F32, tag="o")
-        nc.tensor.matmul(fcb_ps[:], lhsT=ones[:], rhs=vec_rows[:, DIM : DIM + OUT], start=True, stop=True)
+        fcb_ps = psum_o.tile([P, PAIR * OUT], F32, tag="o")
+        nc.tensor.matmul(fcb_ps[:], lhsT=ones[:], rhs=vec_rows[:, DIM : DIM + PAIR * OUT], start=True, stop=True)
 
         gb_ps = psum_z.tile([P, P], BF16, tag="z")
         nc.tensor.transpose(gb_ps[:], gb_rows[:], ident_bf[:])
@@ -130,8 +134,8 @@ def tile_pinmodel_pa_t_kernel(tc, x, km1, b1, t2, core2, t3, core3, ln_g, ln_b, 
         nc.vector.tensor_copy(out=b1_bc[:], in_=b1_ps[:])
         w_grouped = consts.tile([P, OUT, PACK], BF16, align_bytes=64)
         nc.vector.tensor_copy(out=w_grouped[:], in_=w_ps[:].rearrange("p t o -> p o t"))
-        fcb_bc = consts.tile([P, OUT], F32)
-        nc.vector.tensor_copy(out=fcb_bc[:], in_=fcb_ps[:])
+        fcb_bc = consts.tile([P, PAIR, OUT], F32)
+        nc.vector.tensor_copy(out=fcb_bc[:].rearrange("p i o -> p (i o)"), in_=fcb_ps[:])
         gb_col = consts.tile([P, 2 * PACK], F32)
         nc.vector.tensor_copy(out=gb_col[:], in_=gb_ps[:, 0 : 2 * PACK])
         w_codes = consts.tile([P, OUT], U32, align_bytes=64)
@@ -263,74 +267,98 @@ def tile_pinmodel_pa_t_kernel(tc, x, km1, b1, t2, core2, t3, core3, ln_g, ln_b, 
         y_grouped = {}
         y_codes = {}
 
-        def transpose_z(n):
-            if not live(n):
-                return
-            z_banks[n] = psum_z.tile([P, PACK, P], F32, tag="z", name="z_bank")
-            for t in range(PACK):
-                nc.tensor.transpose(z_banks[n][:, t, :], z_tiles[n][:, P * t : P * (t + 1)], ident_f32[:])
+        def live_pair(j):
+            return 0 <= j < TILES // PAIR
 
-        def scale_shift(n, t):
-            if not live(n):
+        def transpose_z(j, h):
+            if not live_pair(j):
+                return
+            z_banks[j, h] = psum_z.tile([P, 2, PAIR, P], F32, tag="z", name="z_bank")
+            for u in range(2):
+                t = 2 * h + u
+                for i in range(PAIR):
+                    nc.tensor.transpose(
+                        z_banks[j, h][:, u, i, :], z_tiles[PAIR * j + i][:, P * t : P * (t + 1)], ident_f32[:]
+                    )
+
+        def scale_shift(j, t):
+            if not live_pair(j):
                 return
             if t == 0:
-                y_planes[n] = work.tile([P, PACK, P], BF16, name="y_planes")
+                y_planes[j] = work.tile([P, PACK, PAIR * P], BF16, name="y_planes")
             nc.scalar.activation(
-                out=y_planes[n][:, t, :], in_=z_banks[n][:, t, :], func=ACT.Identity,
-                scale=gb_col[:, t : t + 1], bias=gb_col[:, PACK + t : PACK + t + 1],
+                out=y_planes[j][:, t, :], in_=z_banks[j, t // 2][:, t % 2, :, :].rearrange("p i r -> p (i r)"),
+                func=ACT.Identity, scale=gb_col[:, t : t + 1], bias=gb_col[:, PACK + t : PACK + t + 1],
             )
 
-        def regroup_y(n):
-            if not live(n):
+        def regroup_y(j):
+            if not live_pair(j):
                 return
-            y_grouped[n] = work.tile([P, P, PACK], BF16, align_bytes=64, name="y_grouped")
-            regroup(nc.vector.tensor_copy, y_grouped[n][:], y_planes[n][:])
+            y_grouped[j] = work.tile([P, PAIR * P, PACK], BF16, align_bytes=64, name="y_grouped")
+            regroup(nc.vector.tensor_copy, y_grouped[j][:], y_planes[j][:])
 
-        def quantise_y(n):
-            if not live(n):
+        def quantise_y(j):
+            if not live_pair(j):
                 return
-            codes = work.tile([P, P], U32, align_bytes=64, name="y_code")
-            scales = work.tile([P, P], U8, align_bytes=64, name="y_scale")
+            codes = work.tile([P, PAIR * P], U32, align_bytes=64, name="y_code")
+            scales = work.tile([P, PAIR * P], U8, align_bytes=64, name="y_scale")
             nc.vector.quantize_mx(
-                out=codes[:].bitcast(FP8X4), scales=scales[:], in_=y_grouped[n][:].rearrange("p r t -> p (r t)")
+                out=codes[:].bitcast(FP8X4), scales=scales[:], in_=y_grouped[j][:].rearrange("p r t -> p (r t)")
             )
-            y_codes[n] = (codes, scales)
+            y_codes[j] = (codes, scales)
 
-        def head(n):
-            if not live(n):
+        fin_banks = {}
+
+        def head(j):
+            if not live_pair(j):
                 return
-            codes, scales = y_codes[n]
-            fin = psum_t.tile([P, OUT], F32, tag="t")
-            nc.tensor.matmul_mx(
-                out=fin[:],
-                lhsT=codes[:].bitcast(FP8X4),
-                lhsT_scale=scales[:],
-                rhs=w_codes[:].bitcast(FP8X4),
-                rhs_scale=w_scales[:],
-                start=True,
-                stop=True,
-            )
-            result = work.tile([P, OUT], F32)
-            nc.vector.tensor_tensor(out=result[:], in0=fin[:], in1=fcb_bc[:], op=ALU.add)
-            nc.sync.dma_start(out=out_rows[:, n, :], in_=result[:])
+            codes, scales = y_codes[j]
+            fin_banks[j] = psum_t.tile([P, PAIR, OUT], F32, tag="t", name="fin")
+            for i in range(PAIR):
+                nc.tensor.matmul_mx(
+                    out=fin_banks[j][:, i, :],
+                    lhsT=codes[:, P * i : P * (i + 1)].bitcast(FP8X4),
+                    lhsT_scale=scales[:, P * i : P * (i + 1)],
+                    rhs=w_codes[:].bitcast(FP8X4),
+                    rhs_scale=w_scales[:],
+                    start=True,
+                    stop=True,
+                )
 
-        for s in range(-4, TILES + 6):
+        def finish(j):
+            if not live_pair(j):
+                return
+            result = work.tile([P, PAIR, OUT], F32)
+            nc.vector.tensor_tensor(out=result[:], in0=fin_banks[j][:], in1=fcb_bc[:], op=ALU.add)
+            nc.sync.dma_start(out=out_rows[:, PAIR * j : PAIR * (j + 1), :], in_=result[:])
+
+        for s in range(-4, TILES + 9):
+            odd = s % 2 == 1
             quantise_t(s)
             add_terms(s - 1)
+            if odd:
+                regroup_y((s - 7) // 2)
+            else:
+                quantise_y((s - 8) // 2)
             normalise(s - 3)
-            regroup_y(s - 5)
             mean(s - 2)
             transpose_t(s + 2)
-            transpose_z(s - 4)
+            if odd:
+                transpose_z((s - 5) // 2, 0)
+            else:
+                transpose_z((s - 6) // 2, 1)
             squares(s - 2)
-            scale_shift(s - 4, 0)
-            scale_shift(s - 4, 1)
+            if odd:
+                scale_shift((s - 5) // 2, 0)
+                scale_shift((s - 5) // 2, 1)
+            else:
+                scale_shift((s - 6) // 2, 2)
+                scale_shift((s - 6) // 2, 3)
             inverse_deviation(s - 2)
-            scale_shift(s - 4, 2)
-            scale_shift(s - 4, 3)
             plain_product(s + 1)
-            quantise_y(s - 5)
-            head(s - 6)
+            if not odd:
+                head((s - 10) // 2)
+                finish((s - 10) // 2)
             mx_products(s)
             if (s + 4) % X_BANK == 0 and live(s + 4):
                 transpose_x((s + 4) // X_BANK)

@@ -226,6 +226,7 @@ def tile_pinmodel_pa_t_kernel(tc, x, km1, b1, t2, core2, t3, core3, ln_g, ln_b, 
         neg_means = {}
         sq_sums = {}
         rstds = {}
+        shifts = {}
 
         def mean(n):
             if not live(n):
@@ -251,15 +252,21 @@ def tile_pinmodel_pa_t_kernel(tc, x, km1, b1, t2, core2, t3, core3, ln_g, ln_b, 
                 out=rstds[n][:], in_=sq_sums[n][:], func=ACT.Abs_reciprocal_sqrt, bias=eps_col[:], scale=1.0 / DIM
             )
 
+        def shift(n):
+            if not live(n):
+                return
+            shifts[n] = work.tile([P, 1], F32, name="shift")
+            nc.scalar.mul(out=shifts[n][:], in_=neg_means[n][:], mul=rstds[n][:])
+
         z_tiles = {}
 
         def normalise(n):
             if not live(n):
                 return
             z_tiles[n] = work.tile([P, DIM], F32, name="z")
-            nc.vector.tensor_scalar(
-                out=z_tiles[n][:], in0=o_tiles[n][:], scalar1=neg_means[n][:], scalar2=rstds[n][:],
-                op0=ALU.add, op1=ALU.mult,
+            nc.gpsimd.tensor_scalar(
+                out=z_tiles[n][:], in0=o_tiles[n][:], scalar1=rstds[n][:], scalar2=shifts[n][:],
+                op0=ALU.mult, op1=ALU.add,
             )
 
         z_banks = {}
@@ -334,14 +341,15 @@ def tile_pinmodel_pa_t_kernel(tc, x, km1, b1, t2, core2, t3, core3, ln_g, ln_b, 
 
         for s in range(-4, TILES + 9):
             odd = s % 2 == 1
-            quantise_t(s)
-            add_terms(s - 1)
+            quantise_t(s + 0)
             if odd:
                 regroup_y((s - 7) // 2)
             else:
                 quantise_y((s - 8) // 2)
-            normalise(s - 3)
+            add_terms(s - 1)
             mean(s - 2)
+            shift(s - 3)
+            normalise(s - 3)
             transpose_t(s + 2)
             if odd:
                 transpose_z((s - 5) // 2, 0)

@@ -63,12 +63,23 @@ def tile_pinmodel_pa_t_kernel(tc, x, km1, b1, t2, core2, t3, core3, ln_g, ln_b, 
         def load_x(i):
             nc.sync.dma_start(out=x_sb[i][:], in_=x_rows[:, X_BANK * i : X_BANK * (i + 1), :])
 
-        for w in range(2):
-            nc.sync.dma_start(out=core_raw[w][:].rearrange("p g (u e) d -> p g u e d", e=2), in_=core_rows[w])
-        t_per_x = T_BUFS * X_BANK // TILES
-        for n in range(T_BUFS):
-            if n % t_per_x == 0:
-                load_x(n // t_per_x)
+        def load_core(w, g):
+            nc.sync.dma_start(
+                out=core_raw[w][:, g].rearrange("p (u e) d -> p u e d", e=2), in_=core_rows[w][:, g]
+            )
+
+        load_core(0, 0)
+        load_core(0, 1)
+        load_core(1, 0)
+        load_core(1, 1)
+        load_t(0)
+        load_x(0)
+        load_t(1)
+        load_t(2)
+        load_t(3)
+        for n in range(4, T_BUFS):
+            if n % 4 == 0:
+                load_x(n // 4)
             load_t(n)
 
         km1_sb = consts.tile([P, DIM], BF16)
@@ -100,7 +111,9 @@ def tile_pinmodel_pa_t_kernel(tc, x, km1, b1, t2, core2, t3, core3, ln_g, ln_b, 
         ones = consts.tile([P, P], BF16)
         nc.vector.memset(ones[:], 1.0)
         eps_col = consts.tile([P, 1], F32)
-        nc.vector.memset(eps_col[:], EPS)
+        nc.vector.memset(eps_col[:], EPS / DIM**2)
+        warm = consts.tile([P, 1], F32)
+        nc.scalar.activation(out=warm[:], in_=eps_col[:], func=ACT.Abs_reciprocal_sqrt, bias=eps_col[:], scale=1.0)
 
         b1_ps = psum_o.tile([P, DIM], F32, tag="o")
         nc.tensor.matmul(b1_ps[:], lhsT=ones[:], rhs=vec_rows[:, 0:DIM], start=True, stop=True)
@@ -114,6 +127,12 @@ def tile_pinmodel_pa_t_kernel(tc, x, km1, b1, t2, core2, t3, core3, ln_g, ln_b, 
         for t in range(PACK):
             nc.tensor.transpose(w_ps[:, t, :], fcw_sb[:, P * t : P * (t + 1)], ident_bf[:])
 
+        b1_bc = consts.tile([P, DIM], F32)
+        w_grouped = consts.tile([P, OUT, PACK], BF16, align_bytes=64)
+        fcb_bc = consts.tile([P, PAIR, OUT], F32)
+        gb_col = consts.tile([P, 2 * PACK], F32)
+        w_codes = consts.tile([P, OUT], U32, align_bytes=64)
+        w_scales = consts.tile([P, OUT], U8, align_bytes=64)
         core_codes = consts.tile([P, PASSES, DIM], U32, align_bytes=64)
         core_scales = consts.tile([P, PASSES, DIM], U8, align_bytes=64)
         for w in range(2):
@@ -123,6 +142,10 @@ def tile_pinmodel_pa_t_kernel(tc, x, km1, b1, t2, core2, t3, core3, ln_g, ln_b, 
             ]
             regroup(nc.vector.tensor_copy, core_grouped[0][:], core_raw[w][:, 0])
             regroup(nc.scalar.copy, core_grouped[1][:], core_raw[w][:, 1])
+            if w == 0:
+                nc.vector.tensor_scalar(out=b1_bc[:], in0=b1_ps[:], scalar1=1.0 / DIM, scalar2=None, op0=ALU.mult)
+            else:
+                nc.vector.tensor_copy(out=fcb_bc[:].rearrange("p i o -> p (i o)"), in_=fcb_ps[:])
             for g in range(2):
                 nc.vector.quantize_mx(
                     out=core_codes[:, 2 * w + g, :].bitcast(FP8X4),
@@ -130,19 +153,13 @@ def tile_pinmodel_pa_t_kernel(tc, x, km1, b1, t2, core2, t3, core3, ln_g, ln_b, 
                     in_=core_grouped[g][:].rearrange("p d t -> p (d t)"),
                 )
 
-        b1_bc = consts.tile([P, DIM], F32)
-        nc.vector.tensor_copy(out=b1_bc[:], in_=b1_ps[:])
-        w_grouped = consts.tile([P, OUT, PACK], BF16, align_bytes=64)
-        nc.vector.tensor_copy(out=w_grouped[:], in_=w_ps[:].rearrange("p t o -> p o t"))
-        fcb_bc = consts.tile([P, PAIR, OUT], F32)
-        nc.vector.tensor_copy(out=fcb_bc[:].rearrange("p i o -> p (i o)"), in_=fcb_ps[:])
-        gb_col = consts.tile([P, 2 * PACK], F32)
-        nc.vector.tensor_copy(out=gb_col[:], in_=gb_ps[:, 0 : 2 * PACK])
-        w_codes = consts.tile([P, OUT], U32, align_bytes=64)
-        w_scales = consts.tile([P, OUT], U8, align_bytes=64)
-        nc.vector.quantize_mx(
-            out=w_codes[:].bitcast(FP8X4), scales=w_scales[:], in_=w_grouped[:].rearrange("p o t -> p (o t)")
-        )
+        def prepare_head():
+            nc.vector.tensor_copy(out=w_grouped[:], in_=w_ps[:].rearrange("p t o -> p o t"))
+            nc.vector.tensor_copy(out=gb_col[:], in_=gb_ps[:, 0 : 2 * PACK])
+            nc.vector.quantize_mx(
+                out=w_codes[:].bitcast(FP8X4), scales=w_scales[:], in_=w_grouped[:].rearrange("p o t -> p (o t)")
+            )
+
 
         xT = [consts.tile([P, X_BANK, P], BF16, name="xT%d" % i) for i in range(TILES // X_BANK)]
 
@@ -190,7 +207,9 @@ def tile_pinmodel_pa_t_kernel(tc, x, km1, b1, t2, core2, t3, core3, ln_g, ln_b, 
             xk = psum_x.tile([P, DIM], F32, tag="x")
             nc.tensor.matmul(xk[:], lhsT=xT[n // X_BANK][:, n % X_BANK, :], rhs=km1_sb[:], start=True, stop=True)
             xkb_tiles[n] = work.tile([P, DIM], F32, name="xkb")
-            nc.vector.tensor_tensor(out=xkb_tiles[n][:], in0=xk[:], in1=b1_bc[:], op=ALU.add)
+            nc.vector.scalar_tensor_tensor(
+                out=xkb_tiles[n][:], in0=xk[:], scalar=1.0 / DIM, in1=b1_bc[:], op0=ALU.mult, op1=ALU.add
+            )
 
         acc_banks = {}
 
@@ -211,28 +230,21 @@ def tile_pinmodel_pa_t_kernel(tc, x, km1, b1, t2, core2, t3, core3, ln_g, ln_b, 
                 )
 
         o_tiles = {}
-        o_sums = {}
+        means = {}
 
         def add_terms(n):
             if not live(n):
                 return
             o_tiles[n] = work.tile([P, DIM], F32, name="o")
-            o_sums[n] = work.tile([P, 1], F32, name="o_sum")
+            means[n] = work.tile([P, 1], F32, name="mean")
             nc.vector.scalar_tensor_tensor(
-                out=o_tiles[n][:], in0=acc_banks[n][:], scalar=0.0, in1=xkb_tiles[n][:], op0=ALU.add, op1=ALU.add,
-                accum_out=o_sums[n][:],
+                out=o_tiles[n][:], in0=acc_banks[n][:], scalar=1.0 / DIM, in1=xkb_tiles[n][:], op0=ALU.mult, op1=ALU.add,
+                accum_out=means[n][:],
             )
 
-        neg_means = {}
         sq_sums = {}
         rstds = {}
         shifts = {}
-
-        def mean(n):
-            if not live(n):
-                return
-            neg_means[n] = work.tile([P, 1], F32, name="neg_mean")
-            nc.scalar.mul(out=neg_means[n][:], in_=o_sums[n][:], mul=-1.0 / DIM)
 
         def squares(n):
             if not live(n):
@@ -240,7 +252,7 @@ def tile_pinmodel_pa_t_kernel(tc, x, km1, b1, t2, core2, t3, core3, ln_g, ln_b, 
             squared = stage.tile([P, DIM], BF16)
             sq_sums[n] = work.tile([P, 1], F32, name="sq_sum")
             nc.scalar.activation(
-                out=squared[:], in_=o_tiles[n][:], func=ACT.Square, bias=neg_means[n][:], scale=1.0,
+                out=squared[:], in_=o_tiles[n][:], func=ACT.Square, bias=means[n][:], scale=-float(DIM),
                 accum_out=sq_sums[n][:],
             )
 
@@ -249,21 +261,24 @@ def tile_pinmodel_pa_t_kernel(tc, x, km1, b1, t2, core2, t3, core3, ln_g, ln_b, 
                 return
             rstds[n] = work.tile([P, 1], F32, name="rstd")
             nc.scalar.activation(
-                out=rstds[n][:], in_=sq_sums[n][:], func=ACT.Abs_reciprocal_sqrt, bias=eps_col[:], scale=1.0 / DIM
+                out=rstds[n][:], in_=sq_sums[n][:], func=ACT.Abs_reciprocal_sqrt, bias=eps_col[:],
+                scale=1.0 / DIM**3,
             )
 
         def shift(n):
             if not live(n):
                 return
             shifts[n] = work.tile([P, 1], F32, name="shift")
-            nc.scalar.mul(out=shifts[n][:], in_=neg_means[n][:], mul=rstds[n][:])
+            nc.gpsimd.tensor_scalar(
+                out=shifts[n][:], in0=means[n][:], scalar1=rstds[n][:], scalar2=-1.0 / DIM, op0=ALU.mult, op1=ALU.mult
+            )
 
         z_tiles = {}
 
         def normalise(n):
             if not live(n):
                 return
-            z_tiles[n] = work.tile([P, DIM], F32, name="z")
+            z_tiles[n] = work.tile([P, DIM], F32, bufs=8, name="z")
             nc.gpsimd.tensor_scalar(
                 out=z_tiles[n][:], in0=o_tiles[n][:], scalar1=rstds[n][:], scalar2=shifts[n][:],
                 op0=ALU.mult, op1=ALU.add,
@@ -339,34 +354,35 @@ def tile_pinmodel_pa_t_kernel(tc, x, km1, b1, t2, core2, t3, core3, ln_g, ln_b, 
             nc.vector.tensor_tensor(out=result[:], in0=fin_banks[j][:], in1=fcb_bc[:], op=ALU.add)
             nc.sync.dma_start(out=out_rows[:, PAIR * j : PAIR * (j + 1), :], in_=result[:])
 
-        for s in range(-4, TILES + 9):
+        for s in range(-4, TILES + 11):
             odd = s % 2 == 1
-            quantise_t(s + 0)
+            quantise_t(s)
             if odd:
-                regroup_y((s - 7) // 2)
+                regroup_y((s - 9) // 2)
             else:
-                quantise_y((s - 8) // 2)
+                quantise_y((s - 10) // 2)
             add_terms(s - 1)
-            mean(s - 2)
             shift(s - 3)
             normalise(s - 3)
             transpose_t(s + 2)
+            if (s + 2) % X_BANK == 0 and live(s + 2):
+                transpose_x((s + 2) // X_BANK)
             if odd:
-                transpose_z((s - 5) // 2, 0)
+                transpose_z((s - 7) // 2, 0)
             else:
-                transpose_z((s - 6) // 2, 1)
+                transpose_z((s - 8) // 2, 1)
             squares(s - 2)
             if odd:
-                scale_shift((s - 5) // 2, 0)
-                scale_shift((s - 5) // 2, 1)
+                scale_shift((s - 7) // 2, 0)
+                scale_shift((s - 7) // 2, 1)
             else:
-                scale_shift((s - 6) // 2, 2)
-                scale_shift((s - 6) // 2, 3)
+                scale_shift((s - 8) // 2, 2)
+                scale_shift((s - 8) // 2, 3)
             inverse_deviation(s - 2)
-            plain_product(s + 1)
+            plain_product(s)
             if not odd:
-                head((s - 10) // 2)
-                finish((s - 10) // 2)
+                head((s - 12) // 2)
+                finish((s - 12) // 2)
             mx_products(s)
-            if (s + 4) % X_BANK == 0 and live(s + 4):
-                transpose_x((s + 4) // X_BANK)
+            if s == 1:
+                prepare_head()

@@ -18,6 +18,7 @@ EPS = 1e-5
 TILES = B // P
 T_BUFS = 16
 X_BANK = 8
+SCALAR_COLS = 192
 PAIR = 2
 PASSES = 2 * KR // (P * PACK)
 
@@ -63,29 +64,29 @@ def tile_pinmodel_pa_t_kernel(tc, x, km1, b1, t2, core2, t3, core3, ln_g, ln_b, 
         def load_x(i):
             nc.sync.dma_start(out=x_sb[i][:], in_=x_rows[:, X_BANK * i : X_BANK * (i + 1), :])
 
+        x_every = T_BUFS * X_BANK // TILES
+
         def load_core(w, g):
             nc.sync.dma_start(
                 out=core_raw[w][:, g].rearrange("p (u e) d -> p u e d", e=2), in_=core_rows[w][:, g]
             )
 
-        load_core(0, 0)
-        load_core(0, 1)
-        load_core(1, 0)
-        load_core(1, 1)
-        load_t(0)
-        load_x(0)
-        load_t(1)
-        load_t(2)
-        load_t(3)
-        for n in range(4, T_BUFS):
-            if n % 4 == 0:
-                load_x(n // 4)
+        for w in range(2):
+            for g in range(2):
+                load_core(w, g)
+        for n in range(T_BUFS):
             load_t(n)
+            if n % x_every == 0:
+                load_x(n // x_every)
 
         km1_sb = consts.tile([P, DIM], BF16)
         nc.scalar.dma_start(out=km1_sb[:], in_=km1.rearrange("i j d -> (i j) d"))
         fcw_sb = consts.tile([P, DIM], BF16)
         nc.scalar.dma_start(out=fcw_sb[:], in_=fc_w)
+        eps_col = consts.tile([P, 1], F32)
+        nc.vector.memset(eps_col[:], EPS / DIM**2)
+        warm = consts.tile([P, 1], F32)
+        nc.scalar.activation(out=warm[:], in_=eps_col[:], func=ACT.Abs_reciprocal_sqrt, bias=eps_col[:], scale=1.0)
         vec_rows = consts.tile([P, DIM + PAIR * OUT], BF16)
         nc.vector.memset(vec_rows[:], 0.0)
         nc.scalar.dma_start(out=vec_rows[0:1, 0:DIM], in_=b1.rearrange("(o n) -> o n", o=1))
@@ -110,56 +111,14 @@ def tile_pinmodel_pa_t_kernel(tc, x, km1, b1, t2, core2, t3, core3, ln_g, ln_b, 
         make_identity(nc, ident_bf[:])
         ones = consts.tile([P, P], BF16)
         nc.vector.memset(ones[:], 1.0)
-        eps_col = consts.tile([P, 1], F32)
-        nc.vector.memset(eps_col[:], EPS / DIM**2)
-        warm = consts.tile([P, 1], F32)
-        nc.scalar.activation(out=warm[:], in_=eps_col[:], func=ACT.Abs_reciprocal_sqrt, bias=eps_col[:], scale=1.0)
-
-        b1_ps = psum_o.tile([P, DIM], F32, tag="o")
-        nc.tensor.matmul(b1_ps[:], lhsT=ones[:], rhs=vec_rows[:, 0:DIM], start=True, stop=True)
-        fcb_ps = psum_o.tile([P, PAIR * OUT], F32, tag="o")
-        nc.tensor.matmul(fcb_ps[:], lhsT=ones[:], rhs=vec_rows[:, DIM : DIM + PAIR * OUT], start=True, stop=True)
-
-        gb_ps = psum_z.tile([P, P], BF16, tag="z")
-        nc.tensor.transpose(gb_ps[:], gb_rows[:], ident_bf[:])
-
-        w_ps = psum_z.tile([P, PACK, OUT], BF16, tag="z")
-        for t in range(PACK):
-            nc.tensor.transpose(w_ps[:, t, :], fcw_sb[:, P * t : P * (t + 1)], ident_bf[:])
-
         b1_bc = consts.tile([P, DIM], F32)
-        w_grouped = consts.tile([P, OUT, PACK], BF16, align_bytes=64)
         fcb_bc = consts.tile([P, PAIR, OUT], F32)
         gb_col = consts.tile([P, 2 * PACK], F32)
+        w_grouped = consts.tile([P, OUT, PACK], BF16, align_bytes=64)
         w_codes = consts.tile([P, OUT], U32, align_bytes=64)
         w_scales = consts.tile([P, OUT], U8, align_bytes=64)
-        core_codes = consts.tile([P, PASSES, DIM], U32, align_bytes=64)
-        core_scales = consts.tile([P, PASSES, DIM], U8, align_bytes=64)
-        for w in range(2):
-            core_grouped = [
-                stage.tile([P, DIM, PACK], BF16, align_bytes=64, tag="core%d" % g, name="core_grouped%d_%d" % (w, g))
-                for g in range(2)
-            ]
-            regroup(nc.vector.tensor_copy, core_grouped[0][:], core_raw[w][:, 0])
-            regroup(nc.scalar.copy, core_grouped[1][:], core_raw[w][:, 1])
-            if w == 0:
-                nc.vector.tensor_scalar(out=b1_bc[:], in0=b1_ps[:], scalar1=1.0 / DIM, scalar2=None, op0=ALU.mult)
-            else:
-                nc.vector.tensor_copy(out=fcb_bc[:].rearrange("p i o -> p (i o)"), in_=fcb_ps[:])
-            for g in range(2):
-                nc.vector.quantize_mx(
-                    out=core_codes[:, 2 * w + g, :].bitcast(FP8X4),
-                    scales=core_scales[:, 2 * w + g, :],
-                    in_=core_grouped[g][:].rearrange("p d t -> p (d t)"),
-                )
-
-        def prepare_head():
-            nc.vector.tensor_copy(out=w_grouped[:], in_=w_ps[:].rearrange("p t o -> p o t"))
-            nc.vector.tensor_copy(out=gb_col[:], in_=gb_ps[:, 0 : 2 * PACK])
-            nc.vector.quantize_mx(
-                out=w_codes[:].bitcast(FP8X4), scales=w_scales[:], in_=w_grouped[:].rearrange("p o t -> p (o t)")
-            )
-
+        core_codes = consts.tile([P, PASSES, DIM], U32, align_bytes=256)
+        core_scales = consts.tile([P, PASSES, DIM], U8, align_bytes=256)
 
         xT = [consts.tile([P, X_BANK, P], BF16, name="xT%d" % i) for i in range(TILES // X_BANK)]
 
@@ -190,8 +149,8 @@ def tile_pinmodel_pa_t_kernel(tc, x, km1, b1, t2, core2, t3, core3, ln_g, ln_b, 
         def quantise_t(n):
             if not live(n):
                 return
-            codes = work.tile([P, PASSES, P], U32, align_bytes=64, name="t_code")
-            scales = work.tile([P, PASSES, P], U8, align_bytes=64, name="t_scale")
+            codes = work.tile([P, PASSES, P], U32, align_bytes=256, name="t_code")
+            scales = work.tile([P, PASSES, P], U8, align_bytes=256, name="t_scale")
             nc.vector.quantize_mx(
                 out=codes[:].rearrange("p c r -> p (c r)").bitcast(FP8X4),
                 scales=scales[:].rearrange("p c r -> p (c r)"),
@@ -354,9 +313,53 @@ def tile_pinmodel_pa_t_kernel(tc, x, km1, b1, t2, core2, t3, core3, ln_g, ln_b, 
             nc.vector.tensor_tensor(out=result[:], in0=fin_banks[j][:], in1=fcb_bc[:], op=ALU.add)
             nc.sync.dma_start(out=out_rows[:, PAIR * j : PAIR * (j + 1), :], in_=result[:])
 
-        for s in range(-4, TILES + 11):
+        b1_ps = psum_o.tile([P, DIM], F32, tag="o")
+        nc.tensor.matmul(b1_ps[:], lhsT=ones[:], rhs=vec_rows[:, 0:DIM], start=True, stop=True)
+        fcb_ps = psum_o.tile([P, PAIR * OUT], F32, tag="o")
+        nc.tensor.matmul(fcb_ps[:], lhsT=ones[:], rhs=vec_rows[:, DIM : DIM + PAIR * OUT], start=True, stop=True)
+
+        gb_ps = psum_z.tile([P, P], BF16, tag="z")
+        nc.tensor.transpose(gb_ps[:], gb_rows[:], ident_bf[:])
+
+        w_ps = psum_z.tile([P, PACK, OUT], BF16, tag="z")
+        for t in range(PACK):
+            nc.tensor.transpose(w_ps[:, t, :], fcw_sb[:, P * t : P * (t + 1)], ident_bf[:])
+
+        for w in range(2):
+            for g in range(2):
+                core_grouped = stage.tile([P, DIM, PACK], BF16, align_bytes=64, bufs=4, name="core_grouped")
+                for copy, cols in (
+                    (nc.scalar.copy, slice(0, SCALAR_COLS)),
+                    (nc.vector.tensor_copy, slice(SCALAR_COLS, DIM)),
+                ):
+                    regroup(copy, core_grouped[:, cols], core_raw[w][:, g, :, cols])
+                if (w, g) == (1, 0):
+                    nc.vector.tensor_scalar(
+                        out=b1_bc[:], in0=b1_ps[:], scalar1=1.0 / DIM, scalar2=None, op0=ALU.mult
+                    )
+                nc.vector.quantize_mx(
+                    out=core_codes[:, 2 * w + g, :].bitcast(FP8X4),
+                    scales=core_scales[:, 2 * w + g, :],
+                    in_=core_grouped[:].rearrange("p d t -> p (d t)"),
+                )
+        transpose_t(0)
+        transpose_x(0)
+        quantise_t(0)
+        nc.vector.tensor_copy(out=fcb_bc[:].rearrange("p i o -> p (i o)"), in_=fcb_ps[:])
+
+        def group_head():
+            nc.vector.tensor_copy(out=w_grouped[:], in_=w_ps[:].rearrange("p t o -> p o t"))
+            nc.vector.tensor_copy(out=gb_col[:], in_=gb_ps[:, 0 : 2 * PACK])
+
+        def quantise_head():
+            nc.vector.quantize_mx(
+                out=w_codes[:].bitcast(FP8X4), scales=w_scales[:], in_=w_grouped[:].rearrange("p o t -> p (o t)")
+            )
+
+        for s in range(-1, TILES + 11):
             odd = s % 2 == 1
-            quantise_t(s)
+            if s > 0:
+                quantise_t(s)
             if odd:
                 regroup_y((s - 9) // 2)
             else:
@@ -384,5 +387,7 @@ def tile_pinmodel_pa_t_kernel(tc, x, km1, b1, t2, core2, t3, core3, ln_g, ln_b, 
                 head((s - 12) // 2)
                 finish((s - 12) // 2)
             mx_products(s)
+            if s == 0:
+                group_head()
             if s == 1:
-                prepare_head()
+                quantise_head()

@@ -358,8 +358,8 @@ def tile_pinmodel_pa_t_kernel(tc, x, km1, b1, t2, core2, t3, core3, ln_g, ln_b, 
 
         for s in range(-1, TILES + 11):
             odd = s % 2 == 1
-            if s > 0:
-                quantise_t(s)
+            if s >= 0:
+                quantise_t(s + 1)
             if odd:
                 regroup_y((s - 9) // 2)
             else:

from contextlib import ExitStack

import concourse.mybir as mybir
from concourse.masks import make_identity

F32 = mybir.dt.float32
BF16 = mybir.dt.bfloat16
U32 = mybir.dt.uint32
U8 = mybir.dt.uint8
FP8X4 = mybir.dt.float8_e4m3fn_x4
ALU = mybir.AluOpType
ACT = mybir.ActivationFunctionType

P = 128
PACK = 4
B, K1, KR, DIM, OUT = 4096, 128, 1024, 512, 128
EPS = 1e-5
TILES = B // P
T_BUFS = 16
X_BANK = 8
SCALAR_COLS = 192
PAIR = 2
PASSES = 2 * KR // (P * PACK)

FLOPS = 2 * B * DIM * (K1 + 2 * KR) + 2 * B * DIM * OUT


def tile_pinmodel_pa_t_kernel(tc, x, km1, b1, t2, core2, t3, core3, ln_g, ln_b, fc_w, fc_b, out):
    nc = tc.nc

    x_rows = x.rearrange("(p n) i j -> p n (i j)", n=TILES)
    t_rows = [t.rearrange("(p n) i j -> p n (i j)", n=TILES) for t in (t2, t3)]
    out_rows = out.rearrange("(p n) o f -> p n (o f)", n=TILES)
    core_rows = [
        c.rearrange("i j d -> (i j) d").rearrange("(g u p e) d -> p g u e d", g=2, u=2, e=2) for c in (core2, core3)
    ]

    with ExitStack() as stack:
        stack.enter_context(tc.manual_schedule())
        consts = stack.enter_context(tc.tile_pool(name="consts", bufs=1))
        t_pool = stack.enter_context(tc.tile_pool(name="t_pool", bufs=T_BUFS))
        stage = stack.enter_context(tc.tile_pool(name="stage", bufs=2))
        work = stack.enter_context(tc.tile_pool(name="work", bufs=4))
        psum_t = stack.enter_context(tc.psum_pool(name="psum_t", bufs=3))
        psum_z = stack.enter_context(tc.psum_pool(name="psum_z", bufs=2))
        psum_o = stack.enter_context(tc.psum_pool(name="psum_o", bufs=2))
        psum_x = stack.enter_context(tc.psum_pool(name="psum_x", bufs=1))

        def live(n):
            return 0 <= n < TILES

        t_raw = {}

        def load_t(n):
            if not live(n):
                return
            for w in range(2):
                t_raw[w, n] = t_pool.tile([P, KR], BF16, tag="t%d" % w, name="t%d_%d" % (w, n))
                nc.sync.dma_start(out=t_raw[w, n][:], in_=t_rows[w][:, n, :])

        core_raw = [consts.tile([P, 2, PACK, DIM], BF16, name="core_raw%d" % w) for w in range(2)]
        x_sb = [consts.tile([P, X_BANK, K1], BF16, name="x_sb%d" % i) for i in range(TILES // X_BANK)]

        def load_x(i):
            nc.sync.dma_start(out=x_sb[i][:], in_=x_rows[:, X_BANK * i : X_BANK * (i + 1), :])

        x_every = T_BUFS * X_BANK // TILES

        def load_core(w, g):
            nc.sync.dma_start(
                out=core_raw[w][:, g].rearrange("p (u e) d -> p u e d", e=2), in_=core_rows[w][:, g]
            )

        for w in range(2):
            for g in range(2):
                load_core(w, g)
        for n in range(T_BUFS):
            load_t(n)
            if n % x_every == 0:
                load_x(n // x_every)

        km1_sb = consts.tile([P, DIM], BF16)
        nc.scalar.dma_start(out=km1_sb[:], in_=km1.rearrange("i j d -> (i j) d"))
        fcw_sb = consts.tile([P, DIM], BF16)
        nc.scalar.dma_start(out=fcw_sb[:], in_=fc_w)
        eps_col = consts.tile([P, 1], F32)
        nc.vector.memset(eps_col[:], EPS / DIM**2)
        warm = consts.tile([P, 1], F32)
        nc.scalar.activation(out=warm[:], in_=eps_col[:], func=ACT.Abs_reciprocal_sqrt, bias=eps_col[:], scale=1.0)
        vec_rows = consts.tile([P, DIM + PAIR * OUT], BF16)
        nc.vector.memset(vec_rows[:], 0.0)
        nc.scalar.dma_start(out=vec_rows[0:1, 0:DIM], in_=b1.rearrange("(o n) -> o n", o=1))
        for i in range(PAIR):
            nc.scalar.dma_start(
                out=vec_rows[0:1, DIM + OUT * i : DIM + OUT * (i + 1)], in_=fc_b.rearrange("(o n) -> o n", o=1)
            )
        gb_rows = consts.tile([P, P], BF16)
        nc.vector.memset(gb_rows[:], 0.0)
        nc.scalar.dma_start(out=gb_rows[0:PACK, :], in_=ln_g.rearrange("(t p) -> t p", p=P))
        nc.scalar.dma_start(out=gb_rows[PACK : 2 * PACK, :], in_=ln_b.rearrange("(t p) -> t p", p=P))

        def regroup(copy, words, planes):
            copy(
                out=words.rearrange("p (c i) t -> p c t i", i=4),
                in_=planes.rearrange("p t (c i) -> p c t i", i=4),
            )

        ident_f32 = consts.tile([P, P], F32)
        make_identity(nc, ident_f32[:])
        ident_bf = consts.tile([P, P], BF16)
        make_identity(nc, ident_bf[:])
        ones = consts.tile([P, P], BF16)
        nc.vector.memset(ones[:], 1.0)
        b1_bc = consts.tile([P, DIM], F32)
        fcb_bc = consts.tile([P, PAIR, OUT], F32)
        gb_col = consts.tile([P, 2 * PACK], F32)
        w_grouped = consts.tile([P, OUT, PACK], BF16, align_bytes=64)
        w_codes = consts.tile([P, OUT], U32, align_bytes=64)
        w_scales = consts.tile([P, OUT], U8, align_bytes=64)
        core_codes = consts.tile([P, PASSES, DIM], U32, align_bytes=256)
        core_scales = consts.tile([P, PASSES, DIM], U8, align_bytes=256)

        xT = [consts.tile([P, X_BANK, P], BF16, name="xT%d" % i) for i in range(TILES // X_BANK)]

        def transpose_x(i):
            x_bank = psum_t.tile([P, X_BANK, P], BF16, tag="t")
            for n in range(X_BANK):
                nc.tensor.transpose(x_bank[:, n, :], x_sb[i][:, n, :], ident_bf[:])
            nc.scalar.copy(out=xT[i][:], in_=x_bank[:])

        t_grouped = {}
        t_codes = {}

        def transpose_t(n):
            if not live(n):
                return
            t_grouped[n] = work.tile([P, 2, 2, P, PACK], BF16, align_bytes=64, name="t_grouped")
            for w in range(2):
                words = t_raw[w, n][:].bitcast(F32)
                t_bank = psum_t.tile([P, 4, P], F32, tag="t")
                for q in range(4):
                    nc.tensor.transpose(t_bank[:, q, :], words[:, P * q : P * (q + 1)], ident_f32[:])
                nc.scalar.copy(
                    out=t_grouped[n][:].bitcast(F32)[:, w],
                    in_=t_bank[:].rearrange("p (g u) r -> p g r u", u=2),
                )
            load_t(n + T_BUFS)

        def quantise_t(n):
            if not live(n):
                return
            codes = work.tile([P, PASSES, P], U32, align_bytes=256, name="t_code")
            scales = work.tile([P, PASSES, P], U8, align_bytes=256, name="t_scale")
            nc.vector.quantize_mx(
                out=codes[:].rearrange("p c r -> p (c r)").bitcast(FP8X4),
                scales=scales[:].rearrange("p c r -> p (c r)"),
                in_=t_grouped[n][:].rearrange("p w g r t -> p (w g r t)"),
            )
            t_codes[n] = (codes, scales)

        xkb_tiles = {}

        def plain_product(n):
            if not live(n):
                return
            xk = psum_x.tile([P, DIM], F32, tag="x")
            nc.tensor.matmul(xk[:], lhsT=xT[n // X_BANK][:, n % X_BANK, :], rhs=km1_sb[:], start=True, stop=True)
            xkb_tiles[n] = work.tile([P, DIM], F32, name="xkb")
            nc.vector.scalar_tensor_tensor(
                out=xkb_tiles[n][:], in0=xk[:], scalar=1.0 / DIM, in1=b1_bc[:], op0=ALU.mult, op1=ALU.add
            )

        acc_banks = {}

        def mx_products(n):
            if not live(n):
                return
            codes, scales = t_codes[n]
            acc_banks[n] = psum_o.tile([P, DIM], F32, tag="o", name="acc")
            for c in range(PASSES):
                nc.tensor.matmul_mx(
                    out=acc_banks[n][:],
                    lhsT=codes[:, c, :].bitcast(FP8X4),
                    lhsT_scale=scales[:, c, :],
                    rhs=core_codes[:, c, :].bitcast(FP8X4),
                    rhs_scale=core_scales[:, c, :],
                    start=(c == 0),
                    stop=(c == PASSES - 1),
                )

        o_tiles = {}
        means = {}

        def add_terms(n):
            if not live(n):
                return
            o_tiles[n] = work.tile([P, DIM], F32, name="o")
            means[n] = work.tile([P, 1], F32, name="mean")
            nc.vector.scalar_tensor_tensor(
                out=o_tiles[n][:], in0=acc_banks[n][:], scalar=1.0 / DIM, in1=xkb_tiles[n][:], op0=ALU.mult, op1=ALU.add,
                accum_out=means[n][:],
            )

        sq_sums = {}
        rstds = {}
        shifts = {}

        def squares(n):
            if not live(n):
                return
            squared = stage.tile([P, DIM], BF16)
            sq_sums[n] = work.tile([P, 1], F32, name="sq_sum")
            nc.scalar.activation(
                out=squared[:], in_=o_tiles[n][:], func=ACT.Square, bias=means[n][:], scale=-float(DIM),
                accum_out=sq_sums[n][:],
            )

        def inverse_deviation(n):
            if not live(n):
                return
            rstds[n] = work.tile([P, 1], F32, name="rstd")
            nc.scalar.activation(
                out=rstds[n][:], in_=sq_sums[n][:], func=ACT.Abs_reciprocal_sqrt, bias=eps_col[:],
                scale=1.0 / DIM**3,
            )

        def shift(n):
            if not live(n):
                return
            shifts[n] = work.tile([P, 1], F32, name="shift")
            nc.gpsimd.tensor_scalar(
                out=shifts[n][:], in0=means[n][:], scalar1=rstds[n][:], scalar2=-1.0 / DIM, op0=ALU.mult, op1=ALU.mult
            )

        z_tiles = {}

        def normalise(n):
            if not live(n):
                return
            z_tiles[n] = work.tile([P, DIM], F32, bufs=8, name="z")
            nc.gpsimd.tensor_scalar(
                out=z_tiles[n][:], in0=o_tiles[n][:], scalar1=rstds[n][:], scalar2=shifts[n][:],
                op0=ALU.mult, op1=ALU.add,
            )

        z_banks = {}
        y_planes = {}
        y_grouped = {}
        y_codes = {}

        def live_pair(j):
            return 0 <= j < TILES // PAIR

        def transpose_z(j, h):
            if not live_pair(j):
                return
            z_banks[j, h] = psum_z.tile([P, 2, PAIR, P], F32, tag="z", name="z_bank")
            for u in range(2):
                t = 2 * h + u
                for i in range(PAIR):
                    nc.tensor.transpose(
                        z_banks[j, h][:, u, i, :], z_tiles[PAIR * j + i][:, P * t : P * (t + 1)], ident_f32[:]
                    )

        def scale_shift(j, t):
            if not live_pair(j):
                return
            if t == 0:
                y_planes[j] = work.tile([P, PACK, PAIR * P], BF16, name="y_planes")
            nc.scalar.activation(
                out=y_planes[j][:, t, :], in_=z_banks[j, t // 2][:, t % 2, :, :].rearrange("p i r -> p (i r)"),
                func=ACT.Identity, scale=gb_col[:, t : t + 1], bias=gb_col[:, PACK + t : PACK + t + 1],
            )

        def regroup_y(j):
            if not live_pair(j):
                return
            y_grouped[j] = work.tile([P, PAIR * P, PACK], BF16, align_bytes=64, name="y_grouped")
            regroup(nc.vector.tensor_copy, y_grouped[j][:], y_planes[j][:])

        def quantise_y(j):
            if not live_pair(j):
                return
            codes = work.tile([P, PAIR * P], U32, align_bytes=64, name="y_code")
            scales = work.tile([P, PAIR * P], U8, align_bytes=64, name="y_scale")
            nc.vector.quantize_mx(
                out=codes[:].bitcast(FP8X4), scales=scales[:], in_=y_grouped[j][:].rearrange("p r t -> p (r t)")
            )
            y_codes[j] = (codes, scales)

        fin_banks = {}

        def head(j):
            if not live_pair(j):
                return
            codes, scales = y_codes[j]
            fin_banks[j] = psum_t.tile([P, PAIR, OUT], F32, tag="t", name="fin")
            for i in range(PAIR):
                nc.tensor.matmul_mx(
                    out=fin_banks[j][:, i, :],
                    lhsT=codes[:, P * i : P * (i + 1)].bitcast(FP8X4),
                    lhsT_scale=scales[:, P * i : P * (i + 1)],
                    rhs=w_codes[:].bitcast(FP8X4),
                    rhs_scale=w_scales[:],
                    start=True,
                    stop=True,
                )

        def finish(j):
            if not live_pair(j):
                return
            result = work.tile([P, PAIR, OUT], F32)
            nc.vector.tensor_tensor(out=result[:], in0=fin_banks[j][:], in1=fcb_bc[:], op=ALU.add)
            nc.sync.dma_start(out=out_rows[:, PAIR * j : PAIR * (j + 1), :], in_=result[:])

        b1_ps = psum_o.tile([P, DIM], F32, tag="o")
        nc.tensor.matmul(b1_ps[:], lhsT=ones[:], rhs=vec_rows[:, 0:DIM], start=True, stop=True)
        fcb_ps = psum_o.tile([P, PAIR * OUT], F32, tag="o")
        nc.tensor.matmul(fcb_ps[:], lhsT=ones[:], rhs=vec_rows[:, DIM : DIM + PAIR * OUT], start=True, stop=True)

        gb_ps = psum_z.tile([P, P], BF16, tag="z")
        nc.tensor.transpose(gb_ps[:], gb_rows[:], ident_bf[:])

        w_ps = psum_z.tile([P, PACK, OUT], BF16, tag="z")
        for t in range(PACK):
            nc.tensor.transpose(w_ps[:, t, :], fcw_sb[:, P * t : P * (t + 1)], ident_bf[:])

        for w in range(2):
            for g in range(2):
                core_grouped = stage.tile([P, DIM, PACK], BF16, align_bytes=64, bufs=4, name="core_grouped")
                for copy, cols in (
                    (nc.scalar.copy, slice(0, SCALAR_COLS)),
                    (nc.vector.tensor_copy, slice(SCALAR_COLS, DIM)),
                ):
                    regroup(copy, core_grouped[:, cols], core_raw[w][:, g, :, cols])
                if (w, g) == (1, 0):
                    nc.vector.tensor_scalar(
                        out=b1_bc[:], in0=b1_ps[:], scalar1=1.0 / DIM, scalar2=None, op0=ALU.mult
                    )
                nc.vector.quantize_mx(
                    out=core_codes[:, 2 * w + g, :].bitcast(FP8X4),
                    scales=core_scales[:, 2 * w + g, :],
                    in_=core_grouped[:].rearrange("p d t -> p (d t)"),
                )
        transpose_t(0)
        transpose_x(0)
        quantise_t(0)
        nc.vector.tensor_copy(out=fcb_bc[:].rearrange("p i o -> p (i o)"), in_=fcb_ps[:])

        def group_head():
            nc.vector.tensor_copy(out=w_grouped[:], in_=w_ps[:].rearrange("p t o -> p o t"))
            nc.vector.tensor_copy(out=gb_col[:], in_=gb_ps[:, 0 : 2 * PACK])

        def quantise_head():
            nc.vector.quantize_mx(
                out=w_codes[:].bitcast(FP8X4), scales=w_scales[:], in_=w_grouped[:].rearrange("p o t -> p (o t)")
            )

        for s in range(-1, TILES + 11):
            odd = s % 2 == 1
            if s >= 0:
                quantise_t(s + 1)
            if odd:
                regroup_y((s - 9) // 2)
            else:
                quantise_y((s - 10) // 2)
            add_terms(s - 1)
            shift(s - 3)
            normalise(s - 3)
            transpose_t(s + 2)
            if (s + 2) % X_BANK == 0 and live(s + 2):
                transpose_x((s + 2) // X_BANK)
            if odd:
                transpose_z((s - 7) // 2, 0)
            else:
                transpose_z((s - 8) // 2, 1)
            squares(s - 2)
            if odd:
                scale_shift((s - 7) // 2, 0)
                scale_shift((s - 7) // 2, 1)
            else:
                scale_shift((s - 8) // 2, 2)
                scale_shift((s - 8) // 2, 3)
            inverse_deviation(s - 2)
            plain_product(s)
            if not odd:
                head((s - 12) // 2)
                finish((s - 12) // 2)
            mx_products(s)
            if s == 0:
                group_head()
            if s == 1:
                quantise_head()
